import numpy as np
import ml_dtypes


def mxq(x, axis, fmt="e4m3"):
    dtype, down = {"e4m3": (ml_dtypes.float8_e4m3fn, 7), "e5m2": (ml_dtypes.float8_e5m2, 14)}[fmt]
    v = np.moveaxis(np.asarray(x, np.float32).astype(ml_dtypes.bfloat16).astype(np.float64), axis, -1)
    blocks = v.reshape(v.shape[:-1] + (-1, 32))
    amax = np.abs(blocks).max(-1, keepdims=True)
    byte = np.maximum(np.where(amax > 0, np.frexp(amax)[1] - 1 + 127, 0) - down, 1)
    scale = np.exp2(byte - 127.0)
    codes = (blocks / scale).astype(np.float32).astype(dtype).astype(np.float64)
    return np.moveaxis((codes * scale).reshape(v.shape), -1, axis)


WIDE = False


def mx_kscale(k):
    if not WIDE:
        return np.ones(k)
    levels = np.array([10, -10, 5, -5, 0])
    a = np.random.permutation(np.resize(levels, k // 512 * 4)).reshape(k // 512, 4)
    idx = np.arange(k)
    return np.exp2(a[idx // 512, idx % 128 // 32])


BF16 = ml_dtypes.bfloat16


def bf(x):
    return np.asarray(x, np.float32).astype(BF16)


def f64(x):
    return np.asarray(x).astype(np.float64)


B, N, F_NODE, F_EDGE, H = 8, 32, 64, 32, 512


def setup_inputs():
    s, t = mx_kscale(H), mx_kscale(H)
    w1 = np.random.standard_normal((3 * H, H)) / np.sqrt(3 * H) * t
    w1[2 * H:] = w1[2 * H:] / s[:, None]
    return {"h": bf(np.random.standard_normal((B, N, H))),
            "e": bf(np.random.standard_normal((B, N, N, H)) * s),
            "adj_mask": bf(np.random.uniform(size=(B, N, N, 1)) < 0.5),
            "W_m1": bf(w1),
            "b_m1": bf(np.random.standard_normal(H) * 0.3 * t),
            "W_m2": bf(np.random.standard_normal((H, H)) * 2.0 / np.sqrt(H * N) / t[:, None]),
            "b_m2": bf(np.random.standard_normal(H) * 0.4 / np.sqrt(N))}


def reference(h, e, adj_mask, W_m1, b_m1, W_m2, b_m2):
    h = f64(h)
    w1 = f64(W_m1)
    hq = mxq(h, 2, "e4m3")
    a_i = hq @ mxq(w1[:H], 0, "e4m3")
    a_j = hq @ mxq(w1[H:2 * H], 0, "e4m3")
    a_e = mxq(f64(e), 3, "e4m3") @ mxq(w1[2 * H:], 0, "e4m3")
    m = a_i[:, :, None, :] + a_j[:, None, :, :] + a_e + f64(b_m1)
    m = np.maximum(m, 0.0)
    m = (mxq(m, 3, "e4m3") @ mxq(f64(W_m2), 0, "e4m3")) + f64(b_m2)
    m = m * f64(adj_mask)
    return m.sum(axis=-2) + h

@@ -1,0 +1,320 @@
+from contextlib import ExitStack
+
+import concourse.mybir as mybir
+from concourse.masks import make_identity
+
+F32 = mybir.dt.float32
+BF16 = mybir.dt.bfloat16
+U32 = mybir.dt.uint32
+U8 = mybir.dt.uint8
+FP8X4 = mybir.dt.float8_e4m3fn_x4
+ACT = mybir.ActivationFunctionType
+ALU = mybir.AluOpType
+
+P = 128
+PACK = 4
+GRAPHS = 8
+NODES = 32
+H = 512
+CHUNKS = H // P
+HALVES = 2
+GRAPHS_PER_HALF = GRAPHS // HALVES
+J_GROUP = 4
+GROUPS = NODES // J_GROUP
+COLS = J_GROUP * P
+
+FLOPS = 2 * (2 * GRAPHS * NODES * H * H + 2 * GRAPHS * NODES * NODES * H * H)
+
+
+def quantise(nc, operand, values):
+    codes, scales = operand
+    nc.vector.quantize_mx(out=codes.bitcast(FP8X4), scales=scales, in_=values)
+
+
+def mx_operand(pool, width, name):
+    codes = pool.tile([P, width], U32, name=name + "_codes", align_bytes=64)
+    scales = pool.tile([P, width], U8, name=name + "_scales", align_bytes=64)
+    return codes, scales
+
+
+def mx_pass(nc, acc, stationary, first, moving, start, stop):
+    nc.tensor.matmul_mx(
+        out=acc,
+        lhsT=stationary[0][:, first : first + P].bitcast(FP8X4),
+        lhsT_scale=stationary[1][:, first : first + P],
+        rhs=moving[0].bitcast(FP8X4),
+        rhs_scale=moving[1],
+        start=start,
+        stop=stop,
+    )
+
+
+def tile_messagepassing_pa_t_kernel(tc, h, e, adj_mask, W_m1, b_m1, W_m2, b_m2, out):
+    nc = tc.nc
+    h_rows = h.flatten_outer_dims()
+    e_rows = e.rearrange("b i j k -> (b i) (j k)")
+    mask_rows = adj_mask.rearrange("b i j o -> (b i) (j o)")
+    mask_flat = adj_mask.rearrange("b i j o -> (b i j o)")
+    out_rows = out.flatten_outer_dims()
+    steps = HALVES * GROUPS
+
+    with ExitStack() as ctx:
+        keep = ctx.enter_context(tc.tile_pool(name="keep", bufs=1))
+        wstage = ctx.enter_context(tc.tile_pool(name="wstage", bufs=2))
+        e_pool = ctx.enter_context(tc.tile_pool(name="e_pool", bufs=12))
+        work = ctx.enter_context(tc.tile_pool(name="work", bufs=3))
+        ps_t = ctx.enter_context(tc.psum_pool(name="ps_t", bufs=2))
+        ps_1 = ctx.enter_context(tc.psum_pool(name="ps_1", bufs=4))
+        ps_2 = ctx.enter_context(tc.psum_pool(name="ps_2", bufs=2))
+        ctx.enter_context(tc.manual_schedule())
+
+        ident_f32 = keep.tile([P, P], F32, name="ident_f32")
+        make_identity(nc, ident_f32[:])
+        ident_bf16 = keep.tile([P, P], BF16, name="ident_bf16")
+        make_identity(nc, ident_bf16[:])
+
+        e_sb = {}
+
+        def load_e(step):
+            half, group = divmod(step, GROUPS)
+            tile_e = e_pool.tile([P, J_GROUP * H], BF16, name="e_sb")
+            nc.sync.dma_start(
+                out=tile_e[:],
+                in_=e_rows[half * P : (half + 1) * P, group * J_GROUP * H : (group + 1) * J_GROUP * H],
+            )
+            e_sb[step] = tile_e
+
+        def load_w1(name, block):
+            raw = keep.tile([P, PACK * H], BF16, name=name + "_raw")
+            nc.sync.dma_start(
+                out=raw[:].rearrange("q (u f) -> q u f", u=2),
+                in_=W_m1[block * H : (block + 1) * H, :].rearrange("(u q s) n -> q u (s n)", u=2, q=P, s=2),
+            )
+            return raw
+
+        def load_mask_all(half):
+            every = keep.tile([P, P * NODES], BF16, name="mask_all%d" % half)
+            nc.sync.dma_start(
+                out=every[:],
+                in_=mask_flat[half * P * NODES : (half + 1) * P * NODES].partition_broadcast(P),
+            )
+            return every
+
+        b1_rows = keep.tile([P, P], BF16, name="b1_rows")
+        nc.vector.memset(b1_rows[:], 0.0)
+        nc.scalar.dma_start(out=b1_rows[0:CHUNKS, :], in_=b_m1.rearrange("(t p) -> t p", p=P))
+        b2_all = keep.tile([P, H], BF16, name="b2_all")
+        nc.scalar.dma_start(out=b2_all[:], in_=b_m2.partition_broadcast(P))
+        mask_pp = []
+        h_sb = []
+        for half in range(HALVES):
+            pp = keep.tile([P, NODES], BF16, name="mask_pp%d" % half)
+            nc.scalar.dma_start(out=pp[:], in_=mask_rows[half * P : (half + 1) * P, :])
+            mask_pp.append(pp)
+            h_tile = keep.tile([P, H], BF16, name="h_sb%d" % half)
+            nc.sync.dma_start(out=h_tile[:], in_=h_rows[half * P : (half + 1) * P, :])
+            h_sb.append(h_tile)
+        w_raw = {}
+        w_raw["w_xj"] = load_w1("w_xj", 1)
+        w_raw["w_xi"] = load_w1("w_xi", 0)
+        load_e(0)
+        w_raw["w_e2"] = load_w1("w_e2", 2)
+        load_e(1)
+        mask_all = [load_mask_all(0)]
+        w_raw["w_m2"] = keep.tile([P, PACK * H], BF16, name="w_m2_raw")
+        nc.sync.dma_start(
+            out=w_raw["w_m2"][:].rearrange("p (t n) -> p t n", t=PACK),
+            in_=W_m2.rearrange("(t p) n -> p t n", p=P),
+        )
+        for step in range(2, GROUPS):
+            load_e(step)
+        mask_all.append(load_mask_all(1))
+        for step in range(GROUPS, steps):
+            load_e(step)
+
+        weights = {}
+        w_grouped = {}
+
+        def regroup_weight(name, engine_copy):
+            grouped = wstage.tile([P, H * PACK], BF16, name="w_grouped", align_bytes=64)
+            engine_copy(
+                out=grouped[:].rearrange("q (c i t) -> q c t i", i=4, t=PACK),
+                in_=w_raw[name][:].rearrange("q (t c i) -> q c t i", t=PACK, i=4),
+            )
+            w_grouped[name] = grouped
+
+        def quantise_weight(name):
+            weights[name] = mx_operand(keep, H, name)
+            quantise(nc, weights[name], w_grouped[name][:])
+
+        b1_ps = ps_t.tile([P, P], BF16, name="b1_ps", tag="transposed")
+        nc.tensor.transpose(b1_ps[:], b1_rows[:], ident_bf16[:])
+        b1_pp = keep.tile([P, CHUNKS], F32, name="b1_pp")
+        nc.vector.tensor_copy(out=b1_pp[:], in_=b1_ps[:, 0:CHUNKS])
+
+        h_grouped = []
+        for half in range(HALVES):
+            h_words = h_sb[half][:].bitcast(F32)
+            h_ps = ps_t.tile([P, 2 * P], F32, name="h_ps", tag="transposed")
+            for u in range(2):
+                nc.tensor.transpose(h_ps[:, u * P : (u + 1) * P], h_words[:, u * P : (u + 1) * P], ident_f32[:])
+            grouped = wstage.tile([P, J_GROUP * P * 2], F32, name="h_grouped", align_bytes=64)
+            for copy in range(J_GROUP):
+                nc.scalar.copy(
+                    out=grouped[:, copy * 2 * P : (copy + 1) * 2 * P].rearrange("p (c u) -> p c u", u=2),
+                    in_=h_ps[:].rearrange("p (u c) -> p c u", u=2),
+                )
+            h_grouped.append(grouped)
+
+        base = []
+        for half in range(HALVES):
+            degree = keep.tile([P, 1], F32, name="degree%d" % half)
+            nc.vector.reduce_sum(out=degree[:], in_=mask_pp[half][:], axis=mybir.AxisListType.X)
+            rows_base = keep.tile([P, H], F32, name="base%d" % half)
+            nc.vector.scalar_tensor_tensor(
+                out=rows_base[:], in0=b2_all[:], scalar=degree[:, 0:1], in1=h_sb[half][:], op0=ALU.mult, op1=ALU.add
+            )
+            base.append(rows_base)
+
+        regroup_weight("w_xj", nc.vector.tensor_copy)
+        regroup_weight("w_xi", nc.scalar.copy)
+        h_mx = [mx_operand(keep, COLS, "h_mx%d" % half) for half in range(HALVES)]
+        quantise(nc, h_mx[0], h_grouped[0][:].bitcast(BF16))
+        quantise_weight("w_xj")
+        quantise(nc, h_mx[1], h_grouped[1][:].bitcast(BF16))
+
+        aj_b1 = keep.tile([P, CHUNKS * HALVES * P], F32, name="aj_b1")
+        for half in range(HALVES):
+            aj_ps = ps_1.tile([P, CHUNKS * P], F32, name="aj_ps", tag="stage1")
+            for t in range(CHUNKS):
+                mx_pass(nc, aj_ps[:, t * P : (t + 1) * P], weights["w_xj"], t * P, (h_mx[half][0][:, 0:P], h_mx[half][1][:, 0:P]), True, True)
+            for t in range(CHUNKS):
+                nc.scalar.activation(
+                    out=aj_b1[:, (t * HALVES + half) * P : (t * HALVES + half + 1) * P],
+                    in_=aj_ps[:, t * P : (t + 1) * P],
+                    func=ACT.Identity,
+                    bias=b1_pp[:, t : t + 1],
+                )
+
+        e_grouped, e_mx, mask_cols, p_ps, pre, r_grouped, r_mx = {}, {}, {}, {}, {}, {}, {}
+        out_ps = [ps_2.tile([P, H], F32, name="out_ps%d" % half, tag="out_ps") for half in range(HALVES)]
+
+        def transpose_e(step):
+            e_words = e_sb[step][:].bitcast(F32)
+            grouped = work.tile([P, COLS * 2], F32, name="e_grouped", align_bytes=64)
+            for pair in range(J_GROUP // 2):
+                e_ps = ps_t.tile([P, 4 * P], F32, name="e_ps", tag="transposed")
+                for block in range(4):
+                    word0 = (pair * 4 + block) * P
+                    nc.tensor.transpose(e_ps[:, block * P : (block + 1) * P], e_words[:, word0 : word0 + P], ident_f32[:])
+                nc.scalar.copy(
+                    out=grouped[:, pair * 4 * P : (pair + 1) * 4 * P].rearrange("p (j c u) -> p j c u", j=2, u=2),
+                    in_=e_ps[:].rearrange("p (j u c) -> p j c u", j=2, u=2),
+                )
+            e_grouped[step] = grouped
+
+        def quantise_e(step):
+            e_mx[step] = mx_operand(work, COLS, "e_mx")
+            quantise(nc, e_mx[step], e_grouped[step][:].bitcast(BF16))
+
+        def lay_out_mask(step):
+            half, group = divmod(step, GROUPS)
+            cols = work.tile([P, COLS], BF16, name="mask_cols")
+            nc.scalar.copy(
+                out=cols[:].rearrange("p (j b i) -> p j b i", j=J_GROUP, b=GRAPHS_PER_HALF),
+                in_=mask_all[half][:]
+                .rearrange("p (b i j) -> p b i j", b=GRAPHS_PER_HALF, i=NODES)[:, :, :, group * J_GROUP : (group + 1) * J_GROUP]
+                .rearrange("p b i j -> p j b i"),
+            )
+            mask_cols[step] = cols
+
+        def stage_1(step):
+            half = step // GROUPS
+            banks = []
+            for t in range(CHUNKS):
+                bank = ps_1.tile([P, COLS], F32, name="p_ps", tag="stage1")
+                mx_pass(nc, bank[:], weights["w_e2"], t * P, (e_mx[step][0][:], e_mx[step][1][:]), True, False)
+                mx_pass(nc, bank[:], weights["w_xi"], t * P, (h_mx[half][0][:], h_mx[half][1][:]), False, True)
+                banks.append(bank)
+            p_ps[step] = banks
+
+        def add_aj(step):
+            half, group = divmod(step, GROUPS)
+            tile_pre = work.tile([P, CHUNKS * COLS], BF16, name="pre")
+            for t in range(CHUNKS):
+                aj = aj_b1[:, (t * HALVES + half) * P : (t * HALVES + half + 1) * P]
+                nc.vector.tensor_tensor(
+                    out=tile_pre[:, t * COLS : (t + 1) * COLS].rearrange("p (j b i) -> p j b i", j=J_GROUP, b=GRAPHS_PER_HALF),
+                    in0=p_ps[step][t][:].rearrange("p (j b i) -> p j b i", j=J_GROUP, b=GRAPHS_PER_HALF),
+                    in1=aj.rearrange("p (b j) -> p b j", b=GRAPHS_PER_HALF)[:, :, group * J_GROUP : (group + 1) * J_GROUP]
+                    .rearrange("p b j -> p j b")
+                    .unsqueeze(3)
+                    .to_broadcast([P, J_GROUP, GRAPHS_PER_HALF, NODES]),
+                    op=ALU.add,
+                )
+            pre[step] = tile_pre
+
+        def apply_mask(step):
+            view = pre[step][:].rearrange("p (t c) -> p t c", t=CHUNKS)
+            nc.vector.tensor_tensor(
+                out=view, in0=view, in1=mask_cols[step][:].unsqueeze(1).to_broadcast([P, CHUNKS, COLS]), op=ALU.mult
+            )
+
+        def relu_and_regroup(step):
+            grouped = work.tile([P, COLS * PACK], BF16, name="r_grouped", align_bytes=64)
+            nc.scalar.activation(
+                out=grouped[:].rearrange("p (c i t) -> p c t i", i=4, t=PACK),
+                in_=pre[step][:].rearrange("p (t c i) -> p c t i", t=PACK, i=4),
+                func=ACT.Relu,
+            )
+            r_grouped[step] = grouped
+
+        def quantise_r(step):
+            r_mx[step] = mx_operand(work, COLS, "r_mx")
+            quantise(nc, r_mx[step], r_grouped[step][:])
+
+        def stage_2(step):
+            half, group = divmod(step, GROUPS)
+            for j in range(J_GROUP):
+                mx_pass(
+                    nc,
+                    out_ps[half][:],
+                    r_mx[step],
+                    j * P,
+                    (weights["w_m2"][0][:], weights["w_m2"][1][:]),
+                    group == 0 and j == 0,
+                    group == GROUPS - 1 and j == J_GROUP - 1,
+                )
+
+        def pipeline_step(s):
+            if 0 <= s:
+                apply_mask(s)
+                relu_and_regroup(s)
+            if s + 3 < steps:
+                transpose_e(s + 3)
+            if 0 <= s + 2 < steps:
+                lay_out_mask(s + 2)
+            if 0 <= s + 1 < steps:
+                add_aj(s + 1)
+            if 0 <= s + 2 < steps:
+                quantise_e(s + 2)
+                stage_1(s + 2)
+            if 0 <= s:
+                quantise_r(s)
+                stage_2(s)
+
+        pipeline_step(-3)
+        regroup_weight("w_e2", nc.vector.tensor_copy)
+        quantise_weight("w_xi")
+        quantise_weight("w_e2")
+        pipeline_step(-2)
+        regroup_weight("w_m2", nc.scalar.copy)
+        pipeline_step(-1)
+        quantise_weight("w_m2")
+        for s in range(steps):
+            pipeline_step(s)
+
+        for half in range(HALVES):
+            result = work.tile([P, H], F32, name="result")
+            nc.vector.tensor_tensor(out=result[:], in0=out_ps[half][:], in1=base[half][:], op=ALU.add)
+            nc.sync.dma_start(out=out_rows[half * P : (half + 1) * P, :], in_=result[:])

@@ -105,6 +105,8 @@ def tile_messagepassing_pa_t_kernel(tc, h, e, adj_mask, W_m1, b_m1, W_m2, b_m2, 
         nc.scalar.dma_start(out=b1_rows[0:CHUNKS, :], in_=b_m1.rearrange("(t p) -> t p", p=P))
         b2_all = keep.tile([P, H], BF16, name="b2_all")
         nc.scalar.dma_start(out=b2_all[:], in_=b_m2.partition_broadcast(P))
+        w_raw = {}
+        w_raw["w_xj"] = load_w1("w_xj", 1)
         mask_pp = []
         h_sb = []
         for half in range(HALVES):
@@ -114,8 +116,6 @@ def tile_messagepassing_pa_t_kernel(tc, h, e, adj_mask, W_m1, b_m1, W_m2, b_m2, 
             h_tile = keep.tile([P, H], BF16, name="h_sb%d" % half)
             nc.sync.dma_start(out=h_tile[:], in_=h_rows[half * P : (half + 1) * P, :])
             h_sb.append(h_tile)
-        w_raw = {}
-        w_raw["w_xj"] = load_w1("w_xj", 1)
         w_raw["w_xi"] = load_w1("w_xi", 0)
         load_e(0)
         w_raw["w_e2"] = load_w1("w_e2", 2)
@@ -167,14 +167,16 @@ def tile_messagepassing_pa_t_kernel(tc, h, e, adj_mask, W_m1, b_m1, W_m2, b_m2, 
             h_grouped.append(grouped)
 
         base = []
-        for half in range(HALVES):
-            degree = keep.tile([P, 1], F32, name="degree%d" % half)
-            nc.vector.reduce_sum(out=degree[:], in_=mask_pp[half][:], axis=mybir.AxisListType.X)
-            rows_base = keep.tile([P, H], F32, name="base%d" % half)
-            nc.vector.scalar_tensor_tensor(
-                out=rows_base[:], in0=b2_all[:], scalar=degree[:, 0:1], in1=h_sb[half][:], op0=ALU.mult, op1=ALU.add
-            )
-            base.append(rows_base)
+
+        def compute_base():
+            for half in range(HALVES):
+                degree = keep.tile([P, 1], F32, name="degree%d" % half)
+                nc.vector.reduce_sum(out=degree[:], in_=mask_pp[half][:], axis=mybir.AxisListType.X)
+                rows_base = keep.tile([P, H], F32, name="base%d" % half)
+                nc.vector.scalar_tensor_tensor(
+                    out=rows_base[:], in0=b2_all[:], scalar=degree[:, 0:1], in1=h_sb[half][:], op0=ALU.mult, op1=ALU.add
+                )
+                base.append(rows_base)
 
         regroup_weight("w_xj", nc.vector.tensor_copy)
         regroup_weight("w_xi", nc.scalar.copy)
@@ -220,11 +222,15 @@ def tile_messagepassing_pa_t_kernel(tc, h, e, adj_mask, W_m1, b_m1, W_m2, b_m2, 
         def lay_out_mask(step):
             half, group = divmod(step, GROUPS)
             cols = work.tile([P, COLS], BF16, name="mask_cols")
-            nc.scalar.copy(
+            nc.gpsimd.tensor_scalar(
                 out=cols[:].rearrange("p (j b i) -> p j b i", j=J_GROUP, b=GRAPHS_PER_HALF),
-                in_=mask_all[half][:]
+                in0=mask_all[half][:]
                 .rearrange("p (b i j) -> p b i j", b=GRAPHS_PER_HALF, i=NODES)[:, :, :, group * J_GROUP : (group + 1) * J_GROUP]
                 .rearrange("p b i j -> p j b i"),
+                scalar1=1.0,
+                scalar2=0.0,
+                op0=ALU.mult,
+                op1=ALU.add,
             )
             mask_cols[step] = cols
 
@@ -296,6 +302,8 @@ def tile_messagepassing_pa_t_kernel(tc, h, e, adj_mask, W_m1, b_m1, W_m2, b_m2, 
                 lay_out_mask(s + 2)
             if 0 <= s + 1 < steps:
                 add_aj(s + 1)
+            if s + 1 == steps:
+                compute_base()
             if 0 <= s + 2 < steps:
                 quantise_e(s + 2)
                 stage_1(s + 2)

@@ -102,20 +102,16 @@ def tile_messagepassing_pa_t_kernel(tc, h, e, adj_mask, W_m1, b_m1, W_m2, b_m2, 
 
         b1_rows = keep.tile([P, P], BF16, name="b1_rows")
         nc.vector.memset(b1_rows[:], 0.0)
-        nc.scalar.dma_start(out=b1_rows[0:CHUNKS, :], in_=b_m1.rearrange("(t p) -> t p", p=P))
         b2_all = keep.tile([P, H], BF16, name="b2_all")
-        nc.scalar.dma_start(out=b2_all[:], in_=b_m2.partition_broadcast(P))
         w_raw = {}
         w_raw["w_xj"] = load_w1("w_xj", 1)
         mask_pp = []
         h_sb = []
         for half in range(HALVES):
-            pp = keep.tile([P, NODES], BF16, name="mask_pp%d" % half)
-            nc.scalar.dma_start(out=pp[:], in_=mask_rows[half * P : (half + 1) * P, :])
-            mask_pp.append(pp)
             h_tile = keep.tile([P, H], BF16, name="h_sb%d" % half)
             nc.sync.dma_start(out=h_tile[:], in_=h_rows[half * P : (half + 1) * P, :])
             h_sb.append(h_tile)
+        nc.sync.dma_start(out=b1_rows[0:CHUNKS, :], in_=b_m1.rearrange("(t p) -> t p", p=P))
         w_raw["w_xi"] = load_w1("w_xi", 0)
         load_e(0)
         w_raw["w_e2"] = load_w1("w_e2", 2)
@@ -131,6 +127,11 @@ def tile_messagepassing_pa_t_kernel(tc, h, e, adj_mask, W_m1, b_m1, W_m2, b_m2, 
         mask_all.append(load_mask_all(1))
         for step in range(GROUPS, steps):
             load_e(step)
+        nc.sync.dma_start(out=b2_all[:], in_=b_m2.partition_broadcast(P))
+        for half in range(HALVES):
+            pp = keep.tile([P, NODES], BF16, name="mask_pp%d" % half)
+            nc.sync.dma_start(out=pp[:], in_=mask_rows[half * P : (half + 1) * P, :])
+            mask_pp.append(pp)
 
         weights = {}
         w_grouped = {}
@@ -147,11 +148,6 @@ def tile_messagepassing_pa_t_kernel(tc, h, e, adj_mask, W_m1, b_m1, W_m2, b_m2, 
             weights[name] = mx_operand(keep, H, name)
             quantise(nc, weights[name], w_grouped[name][:])
 
-        b1_ps = ps_t.tile([P, P], BF16, name="b1_ps", tag="transposed")
-        nc.tensor.transpose(b1_ps[:], b1_rows[:], ident_bf16[:])
-        b1_pp = keep.tile([P, CHUNKS], F32, name="b1_pp")
-        nc.vector.tensor_copy(out=b1_pp[:], in_=b1_ps[:, 0:CHUNKS])
-
         h_grouped = []
         for half in range(HALVES):
             h_words = h_sb[half][:].bitcast(F32)
@@ -159,11 +155,10 @@ def tile_messagepassing_pa_t_kernel(tc, h, e, adj_mask, W_m1, b_m1, W_m2, b_m2, 
             for u in range(2):
                 nc.tensor.transpose(h_ps[:, u * P : (u + 1) * P], h_words[:, u * P : (u + 1) * P], ident_f32[:])
             grouped = wstage.tile([P, J_GROUP * P * 2], F32, name="h_grouped", align_bytes=64)
-            for copy in range(J_GROUP):
-                nc.scalar.copy(
-                    out=grouped[:, copy * 2 * P : (copy + 1) * 2 * P].rearrange("p (c u) -> p c u", u=2),
-                    in_=h_ps[:].rearrange("p (u c) -> p c u", u=2),
-                )
+            nc.scalar.copy(
+                out=grouped[:].rearrange("p (r c u) -> p r c u", r=J_GROUP, u=2),
+                in_=h_ps[:].rearrange("p (u c) -> p c u", u=2).unsqueeze(1).to_broadcast([P, J_GROUP, P, 2]),
+            )
             h_grouped.append(grouped)
 
         base = []
@@ -184,6 +179,11 @@ def tile_messagepassing_pa_t_kernel(tc, h, e, adj_mask, W_m1, b_m1, W_m2, b_m2, 
         quantise(nc, h_mx[0], h_grouped[0][:].bitcast(BF16))
         quantise_weight("w_xj")
         quantise(nc, h_mx[1], h_grouped[1][:].bitcast(BF16))
+
+        b1_ps = ps_t.tile([P, P], BF16, name="b1_ps", tag="transposed")
+        nc.tensor.transpose(b1_ps[:], b1_rows[:], ident_bf16[:])
+        b1_pp = keep.tile([P, CHUNKS], F32, name="b1_pp")
+        nc.vector.tensor_copy(out=b1_pp[:], in_=b1_ps[:, 0:CHUNKS])
 
         aj_b1 = keep.tile([P, CHUNKS * HALVES * P], F32, name="aj_b1")
         for half in range(HALVES):

@@ -307,9 +307,9 @@ def tile_messagepassing_pa_t_kernel(tc, h, e, adj_mask, W_m1, b_m1, W_m2, b_m2, 
             if 0 <= s + 2 < steps:
                 quantise_e(s + 2)
                 stage_1(s + 2)
-            if 0 <= s:
-                quantise_r(s)
-                stage_2(s)
+            if 0 <= s - 1:
+                quantise_r(s - 1)
+                stage_2(s - 1)
 
         pipeline_step(-3)
         regroup_weight("w_e2", nc.vector.tensor_copy)
@@ -321,6 +321,8 @@ def tile_messagepassing_pa_t_kernel(tc, h, e, adj_mask, W_m1, b_m1, W_m2, b_m2, 
         quantise_weight("w_m2")
         for s in range(steps):
             pipeline_step(s)
+        quantise_r(steps - 1)
+        stage_2(steps - 1)
 
         for half in range(HALVES):
             result = work.tile([P, H], F32, name="result")

@@ -22,6 +22,7 @@ GRAPHS_PER_HALF = GRAPHS // HALVES
 J_GROUP = 4
 GROUPS = NODES // J_GROUP
 COLS = J_GROUP * P
+LAST_J = J_GROUP - 1
 
 FLOPS = 2 * (2 * GRAPHS * NODES * H * H + 2 * GRAPHS * NODES * NODES * H * H)
 
@@ -75,13 +76,16 @@ def tile_messagepassing_pa_t_kernel(tc, h, e, adj_mask, W_m1, b_m1, W_m2, b_m2, 
 
         e_sb = {}
 
-        def load_e(step):
+        def load_e(step, pieces=1):
             half, group = divmod(step, GROUPS)
             tile_e = e_pool.tile([P, J_GROUP * H], BF16, name="e_sb")
-            nc.sync.dma_start(
-                out=tile_e[:],
-                in_=e_rows[half * P : (half + 1) * P, group * J_GROUP * H : (group + 1) * J_GROUP * H],
-            )
+            width = J_GROUP * H // pieces
+            for piece in range(pieces):
+                first = group * J_GROUP * H + piece * width
+                nc.sync.dma_start(
+                    out=tile_e[:, piece * width : (piece + 1) * width],
+                    in_=e_rows[half * P : (half + 1) * P, first : first + width],
+                )
             e_sb[step] = tile_e
 
         def load_w1(name, block):
@@ -104,25 +108,31 @@ def tile_messagepassing_pa_t_kernel(tc, h, e, adj_mask, W_m1, b_m1, W_m2, b_m2, 
         nc.vector.memset(b1_rows[:], 0.0)
         b2_all = keep.tile([P, H], BF16, name="b2_all")
         w_raw = {}
-        w_raw["w_xj"] = load_w1("w_xj", 1)
         mask_pp = []
         h_sb = []
-        for half in range(HALVES):
+        mask_all = []
+
+        def load_h(half):
             h_tile = keep.tile([P, H], BF16, name="h_sb%d" % half)
             nc.sync.dma_start(out=h_tile[:], in_=h_rows[half * P : (half + 1) * P, :])
             h_sb.append(h_tile)
+
+        w_raw["w_xj"] = load_w1("w_xj", 1)
+        load_h(0)
         nc.sync.dma_start(out=b1_rows[0:CHUNKS, :], in_=b_m1.rearrange("(t p) -> t p", p=P))
-        w_raw["w_xi"] = load_w1("w_xi", 0)
-        load_e(0)
+        load_e(0, pieces=2)
         w_raw["w_e2"] = load_w1("w_e2", 2)
+        w_raw["w_xi"] = load_w1("w_xi", 0)
         load_e(1)
-        mask_all = [load_mask_all(0)]
+        mask_all.append(load_mask_all(0))
         w_raw["w_m2"] = keep.tile([P, PACK * H], BF16, name="w_m2_raw")
         nc.sync.dma_start(
             out=w_raw["w_m2"][:].rearrange("p (t n) -> p t n", t=PACK),
             in_=W_m2.rearrange("(t p) n -> p t n", p=P),
         )
-        for step in range(2, GROUPS):
+        load_e(2)
+        load_h(1)
+        for step in range(3, GROUPS):
             load_e(step)
         mask_all.append(load_mask_all(1))
         for step in range(GROUPS, steps):
@@ -136,60 +146,51 @@ def tile_messagepassing_pa_t_kernel(tc, h, e, adj_mask, W_m1, b_m1, W_m2, b_m2, 
         weights = {}
         w_grouped = {}
 
-        def regroup_weight(name, engine_copy):
-            grouped = wstage.tile([P, H * PACK], BF16, name="w_grouped", align_bytes=64)
+        def regroup_weight(name, engine_copy, first=0, width=H):
+            if name not in w_grouped:
+                w_grouped[name] = wstage.tile([P, H * PACK], BF16, name="w_grouped", align_bytes=64)
+            columns = slice(first // 4, (first + width) // 4)
             engine_copy(
-                out=grouped[:].rearrange("q (c i t) -> q c t i", i=4, t=PACK),
-                in_=w_raw[name][:].rearrange("q (t c i) -> q c t i", t=PACK, i=4),
+                out=w_grouped[name][:].rearrange("q (c i t) -> q c t i", i=4, t=PACK)[:, columns, :, :],
+                in_=w_raw[name][:].rearrange("q (t c i) -> q c t i", t=PACK, i=4)[:, columns, :, :],
             )
-            w_grouped[name] = grouped
 
         def quantise_weight(name):
             weights[name] = mx_operand(keep, H, name)
             quantise(nc, weights[name], w_grouped[name][:])
 
-        h_grouped = []
-        for half in range(HALVES):
+        h_once, h_grouped, h_once_mx, h_mx = {}, {}, {}, {}
+
+        def transpose_h(half):
             h_words = h_sb[half][:].bitcast(F32)
             h_ps = ps_t.tile([P, 2 * P], F32, name="h_ps", tag="transposed")
             for u in range(2):
                 nc.tensor.transpose(h_ps[:, u * P : (u + 1) * P], h_words[:, u * P : (u + 1) * P], ident_f32[:])
-            grouped = wstage.tile([P, J_GROUP * P * 2], F32, name="h_grouped", align_bytes=64)
+            once = keep.tile([P, 2 * P], F32, name="h_once%d" % half, align_bytes=64)
+            nc.scalar.copy(out=once[:].rearrange("p (c u) -> p c u", u=2), in_=h_ps[:].rearrange("p (u c) -> p c u", u=2))
+            grouped = keep.tile([P, J_GROUP * P * 2], F32, name="h_grouped%d" % half, align_bytes=64)
             nc.scalar.copy(
-                out=grouped[:].rearrange("p (r c u) -> p r c u", r=J_GROUP, u=2),
-                in_=h_ps[:].rearrange("p (u c) -> p c u", u=2).unsqueeze(1).to_broadcast([P, J_GROUP, P, 2]),
+                out=grouped[:].rearrange("p (r w) -> p r w", r=J_GROUP),
+                in_=once[:].unsqueeze(1).to_broadcast([P, J_GROUP, 2 * P]),
             )
-            h_grouped.append(grouped)
+            h_once[half], h_grouped[half] = once, grouped
 
-        base = []
+        def quantise_h_once(half):
+            h_once_mx[half] = mx_operand(keep, P, "h_once_mx%d" % half)
+            quantise(nc, h_once_mx[half], h_once[half][:].bitcast(BF16))
 
-        def compute_base():
-            for half in range(HALVES):
-                degree = keep.tile([P, 1], F32, name="degree%d" % half)
-                nc.vector.reduce_sum(out=degree[:], in_=mask_pp[half][:], axis=mybir.AxisListType.X)
-                rows_base = keep.tile([P, H], F32, name="base%d" % half)
-                nc.vector.scalar_tensor_tensor(
-                    out=rows_base[:], in0=b2_all[:], scalar=degree[:, 0:1], in1=h_sb[half][:], op0=ALU.mult, op1=ALU.add
-                )
-                base.append(rows_base)
-
-        regroup_weight("w_xj", nc.vector.tensor_copy)
-        regroup_weight("w_xi", nc.scalar.copy)
-        h_mx = [mx_operand(keep, COLS, "h_mx%d" % half) for half in range(HALVES)]
-        quantise(nc, h_mx[0], h_grouped[0][:].bitcast(BF16))
-        quantise_weight("w_xj")
-        quantise(nc, h_mx[1], h_grouped[1][:].bitcast(BF16))
-
-        b1_ps = ps_t.tile([P, P], BF16, name="b1_ps", tag="transposed")
-        nc.tensor.transpose(b1_ps[:], b1_rows[:], ident_bf16[:])
-        b1_pp = keep.tile([P, CHUNKS], F32, name="b1_pp")
-        nc.vector.tensor_copy(out=b1_pp[:], in_=b1_ps[:, 0:CHUNKS])
+        def quantise_h(half):
+            h_mx[half] = mx_operand(keep, COLS, "h_mx%d" % half)
+            quantise(nc, h_mx[half], h_grouped[half][:].bitcast(BF16))
 
         aj_b1 = keep.tile([P, CHUNKS * HALVES * P], F32, name="aj_b1")
-        for half in range(HALVES):
-            aj_ps = ps_1.tile([P, CHUNKS * P], F32, name="aj_ps", tag="stage1")
+        b1_pp = keep.tile([P, CHUNKS], F32, name="b1_pp")
+
+        def compute_aj(half, aj_ps):
             for t in range(CHUNKS):
-                mx_pass(nc, aj_ps[:, t * P : (t + 1) * P], weights["w_xj"], t * P, (h_mx[half][0][:, 0:P], h_mx[half][1][:, 0:P]), True, True)
+                mx_pass(
+                    nc, aj_ps[:, t * P : (t + 1) * P], weights["w_xj"], t * P, (h_once_mx[half][0][:], h_once_mx[half][1][:]), True, True
+                )
             for t in range(CHUNKS):
                 nc.scalar.activation(
                     out=aj_b1[:, (t * HALVES + half) * P : (t * HALVES + half + 1) * P],
@@ -197,6 +198,20 @@ def tile_messagepassing_pa_t_kernel(tc, h, e, adj_mask, W_m1, b_m1, W_m2, b_m2, 
                     func=ACT.Identity,
                     bias=b1_pp[:, t : t + 1],
                 )
+
+        base = []
+
+        def compute_base(half):
+            degree = keep.tile([P, 1], F32, name="degree%d" % half)
+            nc.vector.reduce_sum(out=degree[:], in_=mask_pp[half][:], axis=mybir.AxisListType.X)
+            diagonal = keep.tile([P, P], BF16, name="diagonal%d" % half)
+            nc.scalar.activation(out=diagonal[:], in_=ident_bf16[:], func=ACT.Copy, scale=degree[:, 0:1])
+            base_ps = ps_t.tile([P, H], F32, name="base_ps", tag="transposed")
+            nc.tensor.matmul(base_ps[:], lhsT=ident_bf16[:], rhs=h_sb[half][:], start=True, stop=False)
+            nc.tensor.matmul(base_ps[:], lhsT=diagonal[:], rhs=b2_all[:], start=False, stop=True)
+            rows_base = keep.tile([P, H], F32, name="base%d" % half)
+            nc.scalar.copy(out=rows_base[:], in_=base_ps[:])
+            base.append(rows_base)
 
         e_grouped, e_mx, mask_cols, p_ps, pre, r_grouped, r_mx = {}, {}, {}, {}, {}, {}, {}
         out_ps = [ps_2.tile([P, H], F32, name="out_ps%d" % half, tag="out_ps") for half in range(HALVES)]
@@ -260,28 +275,36 @@ def tile_messagepassing_pa_t_kernel(tc, h, e, adj_mask, W_m1, b_m1, W_m2, b_m2, 
                 )
             pre[step] = tile_pre
 
-        def apply_mask(step):
-            view = pre[step][:].rearrange("p (t c) -> p t c", t=CHUNKS)
-            nc.vector.tensor_tensor(
-                out=view, in0=view, in1=mask_cols[step][:].unsqueeze(1).to_broadcast([P, CHUNKS, COLS]), op=ALU.mult
-            )
+        def apply_mask(step, first, width):
+            view = pre[step][:].rearrange("p (t c) -> p t c", t=CHUNKS)[:, :, first : first + width]
+            mask = mask_cols[step][:, first : first + width].unsqueeze(1).to_broadcast([P, CHUNKS, width])
+            nc.vector.tensor_tensor(out=view, in0=view, in1=mask, op=ALU.mult)
 
-        def relu_and_regroup(step):
-            grouped = work.tile([P, COLS * PACK], BF16, name="r_grouped", align_bytes=64)
-            nc.scalar.activation(
-                out=grouped[:].rearrange("p (c i t) -> p c t i", i=4, t=PACK),
-                in_=pre[step][:].rearrange("p (t c i) -> p c t i", t=PACK, i=4),
-                func=ACT.Relu,
-            )
-            r_grouped[step] = grouped
+        def regrouping(step, first, width):
+            if step not in r_grouped:
+                r_grouped[step] = work.tile([P, COLS * PACK], BF16, name="r_grouped", align_bytes=64)
+            out_view = r_grouped[step][:, first * PACK : (first + width) * PACK].rearrange("p (c i t) -> p c t i", i=4, t=PACK)
+            in_view = pre[step][:].rearrange("p (t c i) -> p c t i", t=PACK, i=4)[:, first // 4 : (first + width) // 4, :, :]
+            return out_view, in_view
 
-        def quantise_r(step):
-            r_mx[step] = mx_operand(work, COLS, "r_mx")
-            quantise(nc, r_mx[step], r_grouped[step][:])
+        def relu_on_scalar(step, first, width):
+            out_view, in_view = regrouping(step, first, width)
+            nc.scalar.activation(out=out_view, in_=in_view, func=ACT.Relu)
 
-        def stage_2(step):
+        def relu_on_vector(step, first, width):
+            out_view, in_view = regrouping(step, first, width)
+            nc.vector.tensor_scalar_max(out_view, in_view, 0.0)
+
+        def quantise_r(step, first, width):
+            if step not in r_mx:
+                r_mx[step] = mx_operand(work, COLS, "r_mx")
+            codes, scales = r_mx[step]
+            part = slice(first, first + width)
+            quantise(nc, (codes[:, part], scales[:, part]), r_grouped[step][:, first * PACK : (first + width) * PACK])
+
+        def stage_2(step, js):
             half, group = divmod(step, GROUPS)
-            for j in range(J_GROUP):
+            for j in js:
                 mx_pass(
                     nc,
                     out_ps[half][:],
@@ -289,42 +312,76 @@ def tile_messagepassing_pa_t_kernel(tc, h, e, adj_mask, W_m1, b_m1, W_m2, b_m2, 
                     j * P,
                     (weights["w_m2"][0][:], weights["w_m2"][1][:]),
                     group == 0 and j == 0,
-                    group == GROUPS - 1 and j == J_GROUP - 1,
+                    group == GROUPS - 1 and j == LAST_J,
                 )
 
         def pipeline_step(s):
-            if 0 <= s:
-                apply_mask(s)
-                relu_and_regroup(s)
+            if 0 <= s < steps - 1:
+                apply_mask(s, 0, COLS)
+                relu_on_scalar(s, 0, COLS)
             if s + 3 < steps:
                 transpose_e(s + 3)
+            elif s + 3 - steps in range(HALVES):
+                compute_base(s + 3 - steps)
             if 0 <= s + 2 < steps:
                 lay_out_mask(s + 2)
             if 0 <= s + 1 < steps:
                 add_aj(s + 1)
-            if s + 1 == steps:
-                compute_base()
-            if 0 <= s + 2 < steps:
+            if s + 2 == 0:
+                stage_1(0)
+            elif 0 < s + 2 < steps:
                 quantise_e(s + 2)
                 stage_1(s + 2)
             if 0 <= s - 1:
-                quantise_r(s - 1)
-                stage_2(s - 1)
+                quantise_r(s - 1, 0, COLS)
+                stage_2(s - 1, range(J_GROUP))
 
+        transpose_h(0)
+        b1_ps = ps_t.tile([P, P], BF16, name="b1_ps", tag="transposed")
+        nc.tensor.transpose(b1_ps[:], b1_rows[:], ident_bf16[:])
+        regroup_weight("w_xj", nc.vector.tensor_copy)
+        quantise_h_once(0)
+        quantise_weight("w_xj")
+        nc.vector.tensor_copy(out=b1_pp[:], in_=b1_ps[:, 0:CHUNKS])
         pipeline_step(-3)
+        regroup_weight("w_xi", nc.scalar.copy, 0, H // 2)
+        compute_aj(0, ps_1.tile([P, CHUNKS * P], F32, name="aj_ps0", tag="stage1"))
+        quantise_h(0)
         regroup_weight("w_e2", nc.vector.tensor_copy)
-        quantise_weight("w_xi")
+        regroup_weight("w_xi", nc.vector.tensor_copy, H // 2, H // 2)
         quantise_weight("w_e2")
+        quantise_e(0)
+        quantise_weight("w_xi")
         pipeline_step(-2)
         regroup_weight("w_m2", nc.scalar.copy)
         pipeline_step(-1)
-        quantise_weight("w_m2")
-        for s in range(steps):
-            pipeline_step(s)
-        quantise_r(steps - 1)
-        stage_2(steps - 1)
 
-        for half in range(HALVES):
+        def store_result(half):
             result = work.tile([P, H], F32, name="result")
             nc.vector.tensor_tensor(out=result[:], in0=out_ps[half][:], in1=base[half][:], op=ALU.add)
             nc.sync.dma_start(out=out_rows[half * P : (half + 1) * P, :], in_=result[:])
+
+        for s in range(steps - 1):
+            pipeline_step(s)
+            if s == 0:
+                quantise_weight("w_m2")
+            if s == 2:
+                transpose_h(1)
+            if s == 3:
+                quantise_h_once(1)
+                compute_aj(1, ps_t.tile([P, CHUNKS * P], F32, name="aj_ps1", tag="transposed"))
+                quantise_h(1)
+
+        last = steps - 1
+        apply_mask(last, COLS // 2, COLS // 2)
+        relu_on_scalar(last, COLS // 2, COLS // 2)
+        apply_mask(last, 0, COLS // 2)
+        quantise_r(last - 1, 0, COLS)
+        stage_2(last - 1, range(J_GROUP))
+        relu_on_vector(last, 0, COLS // 2)
+        quantise_r(last, 0, COLS // 2)
+        stage_2(last, (0, 1))
+        quantise_r(last, COLS // 2, COLS // 2)
+        stage_2(last, (2, LAST_J))
+        for half in range(HALVES):
+            store_result(half)

@@ -54,8 +54,7 @@ def tile_messagepassing_pa_t_kernel(tc, h, e, adj_mask, W_m1, b_m1, W_m2, b_m2, 
     nc = tc.nc
     h_rows = h.flatten_outer_dims()
     e_rows = e.rearrange("b i j k -> (b i) (j k)")
-    mask_rows = adj_mask.rearrange("b i j o -> (b i) (j o)")
-    mask_flat = adj_mask.rearrange("b i j o -> (b i j o)")
+    mask_by_row = adj_mask.rearrange("b i j o -> (b i) (j o)")
     out_rows = out.flatten_outer_dims()
     steps = HALVES * GROUPS
 
@@ -66,7 +65,8 @@ def tile_messagepassing_pa_t_kernel(tc, h, e, adj_mask, W_m1, b_m1, W_m2, b_m2, 
         work = ctx.enter_context(tc.tile_pool(name="work", bufs=3))
         ps_t = ctx.enter_context(tc.psum_pool(name="ps_t", bufs=2))
         ps_1 = ctx.enter_context(tc.psum_pool(name="ps_1", bufs=4))
-        ps_2 = ctx.enter_context(tc.psum_pool(name="ps_2", bufs=2))
+        ps_2 = ctx.enter_context(tc.psum_pool(name="ps_2", bufs=1))
+        ps_m = ctx.enter_context(tc.psum_pool(name="ps_m", bufs=1))
         ctx.enter_context(tc.manual_schedule())
 
         ident_f32 = keep.tile([P, P], F32, name="ident_f32")
@@ -96,21 +96,12 @@ def tile_messagepassing_pa_t_kernel(tc, h, e, adj_mask, W_m1, b_m1, W_m2, b_m2, 
             )
             return raw
 
-        def load_mask_all(half):
-            every = keep.tile([P, P * NODES], BF16, name="mask_all%d" % half)
-            nc.sync.dma_start(
-                out=every[:],
-                in_=mask_flat[half * P * NODES : (half + 1) * P * NODES].partition_broadcast(P),
-            )
-            return every
-
         b1_rows = keep.tile([P, P], BF16, name="b1_rows")
         nc.vector.memset(b1_rows[:], 0.0)
         b2_all = keep.tile([P, H], BF16, name="b2_all")
         w_raw = {}
-        mask_pp = []
+        mask_sb = []
         h_sb = []
-        mask_all = []
 
         def load_h(half):
             h_tile = keep.tile([P, H], BF16, name="h_sb%d" % half)
@@ -124,7 +115,10 @@ def tile_messagepassing_pa_t_kernel(tc, h, e, adj_mask, W_m1, b_m1, W_m2, b_m2, 
         w_raw["w_e2"] = load_w1("w_e2", 2)
         w_raw["w_xi"] = load_w1("w_xi", 0)
         load_e(1)
-        mask_all.append(load_mask_all(0))
+        for half in range(HALVES):
+            rows = keep.tile([P, NODES], BF16, name="mask_rows%d" % half)
+            nc.sync.dma_start(out=rows[:], in_=mask_by_row[half * P : (half + 1) * P, :])
+            mask_sb.append(rows)
         w_raw["w_m2"] = keep.tile([P, PACK * H], BF16, name="w_m2_raw")
         nc.sync.dma_start(
             out=w_raw["w_m2"][:].rearrange("p (t n) -> p t n", t=PACK),
@@ -134,14 +128,9 @@ def tile_messagepassing_pa_t_kernel(tc, h, e, adj_mask, W_m1, b_m1, W_m2, b_m2, 
         load_h(1)
         for step in range(3, GROUPS):
             load_e(step)
-        mask_all.append(load_mask_all(1))
         for step in range(GROUPS, steps):
             load_e(step)
         nc.sync.dma_start(out=b2_all[:], in_=b_m2.partition_broadcast(P))
-        for half in range(HALVES):
-            pp = keep.tile([P, NODES], BF16, name="mask_pp%d" % half)
-            nc.sync.dma_start(out=pp[:], in_=mask_rows[half * P : (half + 1) * P, :])
-            mask_pp.append(pp)
 
         weights = {}
         w_grouped = {}
@@ -203,7 +192,7 @@ def tile_messagepassing_pa_t_kernel(tc, h, e, adj_mask, W_m1, b_m1, W_m2, b_m2, 
 
         def compute_base(half):
             degree = keep.tile([P, 1], F32, name="degree%d" % half)
-            nc.vector.reduce_sum(out=degree[:], in_=mask_pp[half][:], axis=mybir.AxisListType.X)
+            nc.vector.reduce_sum(out=degree[:], in_=mask_sb[half][:], axis=mybir.AxisListType.X)
             diagonal = keep.tile([P, P], BF16, name="diagonal%d" % half)
             nc.scalar.activation(out=diagonal[:], in_=ident_bf16[:], func=ACT.Copy, scale=degree[:, 0:1])
             base_ps = ps_t.tile([P, H], F32, name="base_ps", tag="transposed")
@@ -214,7 +203,7 @@ def tile_messagepassing_pa_t_kernel(tc, h, e, adj_mask, W_m1, b_m1, W_m2, b_m2, 
             base.append(rows_base)
 
         e_grouped, e_mx, mask_cols, p_ps, pre, r_grouped, r_mx = {}, {}, {}, {}, {}, {}, {}
-        out_ps = [ps_2.tile([P, H], F32, name="out_ps%d" % half, tag="out_ps") for half in range(HALVES)]
+        out_ps = {}
 
         def transpose_e(step):
             e_words = e_sb[step][:].bitcast(F32)
@@ -236,17 +225,18 @@ def tile_messagepassing_pa_t_kernel(tc, h, e, adj_mask, W_m1, b_m1, W_m2, b_m2, 
 
         def lay_out_mask(step):
             half, group = divmod(step, GROUPS)
+            mask_ps = ps_m.tile([P, COLS], BF16, name="mask_ps")
+            for j in range(J_GROUP):
+                source = group * J_GROUP + j
+                nc.tensor.matmul(
+                    mask_ps[:, j * P : (j + 1) * P],
+                    lhsT=mask_sb[half][:, source : source + 1].to_broadcast([P, P]),
+                    rhs=ident_bf16[:],
+                    start=True,
+                    stop=True,
+                )
             cols = work.tile([P, COLS], BF16, name="mask_cols")
-            nc.gpsimd.tensor_scalar(
-                out=cols[:].rearrange("p (j b i) -> p j b i", j=J_GROUP, b=GRAPHS_PER_HALF),
-                in0=mask_all[half][:]
-                .rearrange("p (b i j) -> p b i j", b=GRAPHS_PER_HALF, i=NODES)[:, :, :, group * J_GROUP : (group + 1) * J_GROUP]
-                .rearrange("p b i j -> p j b i"),
-                scalar1=1.0,
-                scalar2=0.0,
-                op0=ALU.mult,
-                op1=ALU.add,
-            )
+            nc.scalar.copy(out=cols[:], in_=mask_ps[:])
             mask_cols[step] = cols
 
         def stage_1(step):
@@ -304,6 +294,8 @@ def tile_messagepassing_pa_t_kernel(tc, h, e, adj_mask, W_m1, b_m1, W_m2, b_m2, 
 
         def stage_2(step, js):
             half, group = divmod(step, GROUPS)
+            if half not in out_ps:
+                out_ps[half] = ps_2.tile([P, H], F32, name="out_ps%d" % half, tag="out_ps")
             for j in js:
                 mx_pass(
                     nc,
@@ -356,9 +348,11 @@ def tile_messagepassing_pa_t_kernel(tc, h, e, adj_mask, W_m1, b_m1, W_m2, b_m2, 
         regroup_weight("w_m2", nc.scalar.copy)
         pipeline_step(-1)
 
-        def store_result(half):
+        sum_0 = keep.tile([P, H], F32, name="sum_0")
+
+        def store_result(half, total):
             result = work.tile([P, H], F32, name="result")
-            nc.vector.tensor_tensor(out=result[:], in0=out_ps[half][:], in1=base[half][:], op=ALU.add)
+            nc.vector.tensor_tensor(out=result[:], in0=total, in1=base[half][:], op=ALU.add)
             nc.sync.dma_start(out=out_rows[half * P : (half + 1) * P, :], in_=result[:])
 
         for s in range(steps - 1):
@@ -367,6 +361,8 @@ def tile_messagepassing_pa_t_kernel(tc, h, e, adj_mask, W_m1, b_m1, W_m2, b_m2, 
                 quantise_weight("w_m2")
             if s == 2:
                 transpose_h(1)
+            if s == GROUPS:
+                nc.scalar.copy(out=sum_0[:], in_=out_ps[0][:])
             if s == 3:
                 quantise_h_once(1)
                 compute_aj(1, ps_t.tile([P, CHUNKS * P], F32, name="aj_ps1", tag="transposed"))
@@ -383,5 +379,5 @@ def tile_messagepassing_pa_t_kernel(tc, h, e, adj_mask, W_m1, b_m1, W_m2, b_m2, 
         stage_2(last, (0, 1))
         quantise_r(last, COLS // 2, COLS // 2)
         stage_2(last, (2, LAST_J))
-        for half in range(HALVES):
-            store_result(half)
+        store_result(0, sum_0[:])
+        store_result(1, out_ps[1][:])

@@ -23,6 +23,7 @@ J_GROUP = 4
 GROUPS = NODES // J_GROUP
 COLS = J_GROUP * P
 LAST_J = J_GROUP - 1
+STEPS_MASKED_BY_TENSOR = 4
 
 FLOPS = 2 * (2 * GRAPHS * NODES * H * H + 2 * GRAPHS * NODES * NODES * H * H)
 
@@ -100,7 +101,9 @@ def tile_messagepassing_pa_t_kernel(tc, h, e, adj_mask, W_m1, b_m1, W_m2, b_m2, 
         nc.vector.memset(b1_rows[:], 0.0)
         b2_all = keep.tile([P, H], BF16, name="b2_all")
         w_raw = {}
-        mask_sb = []
+        mask_in = keep.tile([P, P], BF16, name="mask_in")
+        nc.vector.memset(mask_in[:], 0.0)
+        mask_wide = []
         h_sb = []
 
         def load_h(half):
@@ -114,11 +117,11 @@ def tile_messagepassing_pa_t_kernel(tc, h, e, adj_mask, W_m1, b_m1, W_m2, b_m2, 
         load_e(0, pieces=2)
         w_raw["w_e2"] = load_w1("w_e2", 2)
         w_raw["w_xi"] = load_w1("w_xi", 0)
-        load_e(1)
         for half in range(HALVES):
-            rows = keep.tile([P, NODES], BF16, name="mask_rows%d" % half)
-            nc.sync.dma_start(out=rows[:], in_=mask_by_row[half * P : (half + 1) * P, :])
-            mask_sb.append(rows)
+            nc.sync.dma_start(
+                out=mask_in[:, half * NODES : (half + 1) * NODES], in_=mask_by_row[half * P : (half + 1) * P, :]
+            )
+        load_e(1)
         w_raw["w_m2"] = keep.tile([P, PACK * H], BF16, name="w_m2_raw")
         nc.sync.dma_start(
             out=w_raw["w_m2"][:].rearrange("p (t n) -> p t n", t=PACK),
@@ -126,11 +129,28 @@ def tile_messagepassing_pa_t_kernel(tc, h, e, adj_mask, W_m1, b_m1, W_m2, b_m2, 
         )
         load_e(2)
         load_h(1)
-        for step in range(3, GROUPS):
+        for step in range(3, GROUPS - 2):
             load_e(step)
-        for step in range(GROUPS, steps):
-            load_e(step)
-        nc.sync.dma_start(out=b2_all[:], in_=b_m2.partition_broadcast(P))
+
+        def spread_mask():
+            mask_t_ps = ps_m.tile([P, P], BF16, name="mask_t_ps", tag="mask")
+            nc.tensor.transpose(mask_t_ps[:], mask_in[:], ident_bf16[:])
+            mask_t = keep.tile([P, P], BF16, name="mask_t")
+            nc.scalar.copy(out=mask_t[:], in_=mask_t_ps[:])
+            words = NODES * P // 2
+            parked = out.rearrange("b i k -> (b i k)")[0 : HALVES * words]
+            nc.sync.dma_start(
+                out=parked.rearrange("(r w) -> r w", w=P // 2), in_=mask_t[0 : HALVES * NODES, :].bitcast(F32)
+            )
+            for step in range(GROUPS - 2, GROUPS):
+                load_e(step)
+            for half in range(HALVES):
+                wide = keep.tile([P, words], F32, name="mask_wide%d" % half)
+                nc.sync.dma_start(out=wide[:], in_=parked[half * words : (half + 1) * words].partition_broadcast(P))
+                mask_wide.append(wide)
+            for step in range(GROUPS, steps):
+                load_e(step)
+            nc.sync.dma_start(out=b2_all[:], in_=b_m2.partition_broadcast(P))
 
         weights = {}
         w_grouped = {}
@@ -188,16 +208,19 @@ def tile_messagepassing_pa_t_kernel(tc, h, e, adj_mask, W_m1, b_m1, W_m2, b_m2, 
                     bias=b1_pp[:, t : t + 1],
                 )
 
-        base = []
+        base, diagonals = [], []
 
-        def compute_base(half):
+        def compute_diagonal(half):
             degree = keep.tile([P, 1], F32, name="degree%d" % half)
-            nc.vector.reduce_sum(out=degree[:], in_=mask_sb[half][:], axis=mybir.AxisListType.X)
+            nc.vector.reduce_sum(out=degree[:], in_=mask_in[:, half * NODES : (half + 1) * NODES], axis=mybir.AxisListType.X)
             diagonal = keep.tile([P, P], BF16, name="diagonal%d" % half)
             nc.scalar.activation(out=diagonal[:], in_=ident_bf16[:], func=ACT.Copy, scale=degree[:, 0:1])
+            diagonals.append(diagonal)
+
+        def compute_base(half):
             base_ps = ps_t.tile([P, H], F32, name="base_ps", tag="transposed")
             nc.tensor.matmul(base_ps[:], lhsT=ident_bf16[:], rhs=h_sb[half][:], start=True, stop=False)
-            nc.tensor.matmul(base_ps[:], lhsT=diagonal[:], rhs=b2_all[:], start=False, stop=True)
+            nc.tensor.matmul(base_ps[:], lhsT=diagonals[half][:], rhs=b2_all[:], start=False, stop=True)
             rows_base = keep.tile([P, H], F32, name="base%d" % half)
             nc.scalar.copy(out=rows_base[:], in_=base_ps[:])
             base.append(rows_base)
@@ -225,19 +248,22 @@ def tile_messagepassing_pa_t_kernel(tc, h, e, adj_mask, W_m1, b_m1, W_m2, b_m2, 
 
         def lay_out_mask(step):
             half, group = divmod(step, GROUPS)
-            mask_ps = ps_m.tile([P, COLS], BF16, name="mask_ps")
+            if step >= STEPS_MASKED_BY_TENSOR:
+                mask_cols[step] = mask_wide[half][:].bitcast(BF16)[:, group * COLS : (group + 1) * COLS]
+                return
+            mask_ps = ps_m.tile([P, COLS], BF16, name="mask_ps", tag="mask")
             for j in range(J_GROUP):
-                source = group * J_GROUP + j
+                source = half * NODES + group * J_GROUP + j
                 nc.tensor.matmul(
                     mask_ps[:, j * P : (j + 1) * P],
-                    lhsT=mask_sb[half][:, source : source + 1].to_broadcast([P, P]),
+                    lhsT=mask_in[:, source : source + 1].to_broadcast([P, P]),
                     rhs=ident_bf16[:],
                     start=True,
                     stop=True,
                 )
             cols = work.tile([P, COLS], BF16, name="mask_cols")
             nc.scalar.copy(out=cols[:], in_=mask_ps[:])
-            mask_cols[step] = cols
+            mask_cols[step] = cols[:]
 
         def stage_1(step):
             half = step // GROUPS
@@ -249,10 +275,30 @@ def tile_messagepassing_pa_t_kernel(tc, h, e, adj_mask, W_m1, b_m1, W_m2, b_m2, 
                 banks.append(bank)
             p_ps[step] = banks
 
+        def scalar_adds(step):
+            return step % 2 == 1 and step < steps - 1
+
+        def add_aj_on_scalar(step):
+            half, group = divmod(step, GROUPS)
+            pre[step] = work.tile([P, CHUNKS * COLS], BF16, name="pre")
+            if not scalar_adds(step):
+                return
+            t = 0
+            for j in range(J_GROUP):
+                for b in range(GRAPHS_PER_HALF):
+                    run = slice((j * GRAPHS_PER_HALF + b) * NODES, (j * GRAPHS_PER_HALF + b + 1) * NODES)
+                    source = (t * HALVES + half) * P + b * NODES + group * J_GROUP + j
+                    nc.scalar.activation(
+                        out=pre[step][:, t * COLS : (t + 1) * COLS][:, run],
+                        in_=p_ps[step][t][:, run],
+                        func=ACT.Identity,
+                        bias=aj_b1[:, source : source + 1],
+                    )
+
         def add_aj(step):
             half, group = divmod(step, GROUPS)
-            tile_pre = work.tile([P, CHUNKS * COLS], BF16, name="pre")
-            for t in range(CHUNKS):
+            tile_pre = pre[step]
+            for t in range(1 if scalar_adds(step) else 0, CHUNKS):
                 aj = aj_b1[:, (t * HALVES + half) * P : (t * HALVES + half + 1) * P]
                 nc.vector.tensor_tensor(
                     out=tile_pre[:, t * COLS : (t + 1) * COLS].rearrange("p (j b i) -> p j b i", j=J_GROUP, b=GRAPHS_PER_HALF),
@@ -263,7 +309,6 @@ def tile_messagepassing_pa_t_kernel(tc, h, e, adj_mask, W_m1, b_m1, W_m2, b_m2, 
                     .to_broadcast([P, J_GROUP, GRAPHS_PER_HALF, NODES]),
                     op=ALU.add,
                 )
-            pre[step] = tile_pre
 
         def apply_mask(step, first, width):
             view = pre[step][:].rearrange("p (t c) -> p t c", t=CHUNKS)[:, :, first : first + width]
@@ -308,6 +353,8 @@ def tile_messagepassing_pa_t_kernel(tc, h, e, adj_mask, W_m1, b_m1, W_m2, b_m2, 
                 )
 
         def pipeline_step(s):
+            if 0 <= s + 1 < steps:
+                add_aj_on_scalar(s + 1)
             if 0 <= s < steps - 1:
                 apply_mask(s, 0, COLS)
                 relu_on_scalar(s, 0, COLS)
@@ -344,6 +391,7 @@ def tile_messagepassing_pa_t_kernel(tc, h, e, adj_mask, W_m1, b_m1, W_m2, b_m2, 
         quantise_weight("w_e2")
         quantise_e(0)
         quantise_weight("w_xi")
+        spread_mask()
         pipeline_step(-2)
         regroup_weight("w_m2", nc.scalar.copy)
         pipeline_step(-1)
@@ -361,9 +409,12 @@ def tile_messagepassing_pa_t_kernel(tc, h, e, adj_mask, W_m1, b_m1, W_m2, b_m2, 
                 quantise_weight("w_m2")
             if s == 2:
                 transpose_h(1)
+            if s == GROUPS + 1:
+                for half in range(HALVES):
+                    compute_diagonal(half)
             if s == GROUPS:
                 nc.scalar.copy(out=sum_0[:], in_=out_ps[0][:])
-            if s == 3:
+            if s == 4:
                 quantise_h_once(1)
                 compute_aj(1, ps_t.tile([P, CHUNKS * P], F32, name="aj_ps1", tag="transposed"))
                 quantise_h(1)

@@ -114,8 +114,8 @@ def tile_messagepassing_pa_t_kernel(tc, h, e, adj_mask, W_m1, b_m1, W_m2, b_m2, 
         w_raw["w_xj"] = load_w1("w_xj", 1)
         load_h(0)
         nc.sync.dma_start(out=b1_rows[0:CHUNKS, :], in_=b_m1.rearrange("(t p) -> t p", p=P))
-        load_e(0, pieces=2)
         w_raw["w_e2"] = load_w1("w_e2", 2)
+        load_e(0, pieces=2)
         w_raw["w_xi"] = load_w1("w_xi", 0)
         for half in range(HALVES):
             nc.sync.dma_start(
@@ -276,7 +276,7 @@ def tile_messagepassing_pa_t_kernel(tc, h, e, adj_mask, W_m1, b_m1, W_m2, b_m2, 
             p_ps[step] = banks
 
         def scalar_adds(step):
-            return step % 2 == 1 and step < steps - 1
+            return step % 4 == 2
 
         def add_aj_on_scalar(step):
             half, group = divmod(step, GROUPS)
@@ -375,20 +375,21 @@ def tile_messagepassing_pa_t_kernel(tc, h, e, adj_mask, W_m1, b_m1, W_m2, b_m2, 
                 quantise_r(s - 1, 0, COLS)
                 stage_2(s - 1, range(J_GROUP))
 
+        regroup_weight("w_xj", nc.scalar.copy, 0, H // 2)
         transpose_h(0)
         b1_ps = ps_t.tile([P, P], BF16, name="b1_ps", tag="transposed")
         nc.tensor.transpose(b1_ps[:], b1_rows[:], ident_bf16[:])
-        regroup_weight("w_xj", nc.vector.tensor_copy)
-        quantise_h_once(0)
+        regroup_weight("w_xj", nc.vector.tensor_copy, H // 2, H // 2)
         quantise_weight("w_xj")
+        quantise_h_once(0)
         nc.vector.tensor_copy(out=b1_pp[:], in_=b1_ps[:, 0:CHUNKS])
+        regroup_weight("w_e2", nc.vector.tensor_copy)
         pipeline_step(-3)
         regroup_weight("w_xi", nc.scalar.copy, 0, H // 2)
         compute_aj(0, ps_1.tile([P, CHUNKS * P], F32, name="aj_ps0", tag="stage1"))
         quantise_h(0)
-        regroup_weight("w_e2", nc.vector.tensor_copy)
-        regroup_weight("w_xi", nc.vector.tensor_copy, H // 2, H // 2)
         quantise_weight("w_e2")
+        regroup_weight("w_xi", nc.vector.tensor_copy, H // 2, H // 2)
         quantise_e(0)
         quantise_weight("w_xi")
         spread_mask()
@@ -398,10 +399,13 @@ def tile_messagepassing_pa_t_kernel(tc, h, e, adj_mask, W_m1, b_m1, W_m2, b_m2, 
 
         sum_0 = keep.tile([P, H], F32, name="sum_0")
 
-        def store_result(half, total):
-            result = work.tile([P, H], F32, name="result")
-            nc.vector.tensor_tensor(out=result[:], in0=total, in1=base[half][:], op=ALU.add)
-            nc.sync.dma_start(out=out_rows[half * P : (half + 1) * P, :], in_=result[:])
+        def store_result(half, total, pieces):
+            width = H // pieces
+            for piece in range(pieces):
+                part = slice(piece * width, (piece + 1) * width)
+                result = work.tile([P, width], F32, name="result%d" % half)
+                nc.vector.tensor_tensor(out=result[:], in0=total[:, part], in1=base[half][:, part], op=ALU.add)
+                nc.sync.dma_start(out=out_rows[half * P : (half + 1) * P, part], in_=result[:])
 
         for s in range(steps - 1):
             pipeline_step(s)
@@ -421,14 +425,16 @@ def tile_messagepassing_pa_t_kernel(tc, h, e, adj_mask, W_m1, b_m1, W_m2, b_m2, 
 
         last = steps - 1
         apply_mask(last, COLS // 2, COLS // 2)
-        relu_on_scalar(last, COLS // 2, COLS // 2)
+        for j in (2, LAST_J):
+            relu_on_scalar(last, j * P, P)
         apply_mask(last, 0, COLS // 2)
         quantise_r(last - 1, 0, COLS)
         stage_2(last - 1, range(J_GROUP))
         relu_on_vector(last, 0, COLS // 2)
         quantise_r(last, 0, COLS // 2)
         stage_2(last, (0, 1))
-        quantise_r(last, COLS // 2, COLS // 2)
-        stage_2(last, (2, LAST_J))
-        store_result(0, sum_0[:])
-        store_result(1, out_ps[1][:])
+        for j in (2, LAST_J):
+            quantise_r(last, j * P, P)
+            stage_2(last, (j,))
+        store_result(0, sum_0, 1)
+        store_result(1, out_ps[1], 2)

@@ -23,7 +23,6 @@ J_GROUP = 4
 GROUPS = NODES // J_GROUP
 COLS = J_GROUP * P
 LAST_J = J_GROUP - 1
-STEPS_MASKED_BY_TENSOR = 4
 
 FLOPS = 2 * (2 * GRAPHS * NODES * H * H + 2 * GRAPHS * NODES * NODES * H * H)
 
@@ -62,7 +61,7 @@ def tile_messagepassing_pa_t_kernel(tc, h, e, adj_mask, W_m1, b_m1, W_m2, b_m2, 
     with ExitStack() as ctx:
         keep = ctx.enter_context(tc.tile_pool(name="keep", bufs=1))
         wstage = ctx.enter_context(tc.tile_pool(name="wstage", bufs=2))
-        e_pool = ctx.enter_context(tc.tile_pool(name="e_pool", bufs=12))
+        e_pool = ctx.enter_context(tc.tile_pool(name="e_pool", bufs=16))
         work = ctx.enter_context(tc.tile_pool(name="work", bufs=3))
         ps_t = ctx.enter_context(tc.psum_pool(name="ps_t", bufs=2))
         ps_1 = ctx.enter_context(tc.psum_pool(name="ps_1", bufs=4))
@@ -103,7 +102,6 @@ def tile_messagepassing_pa_t_kernel(tc, h, e, adj_mask, W_m1, b_m1, W_m2, b_m2, 
         w_raw = {}
         mask_in = keep.tile([P, P], BF16, name="mask_in")
         nc.vector.memset(mask_in[:], 0.0)
-        mask_wide = []
         h_sb = []
 
         def load_h(half):
@@ -112,7 +110,8 @@ def tile_messagepassing_pa_t_kernel(tc, h, e, adj_mask, W_m1, b_m1, W_m2, b_m2, 
             h_sb.append(h_tile)
 
         w_raw["w_xj"] = load_w1("w_xj", 1)
-        load_h(0)
+        for half in range(HALVES):
+            load_h(half)
         nc.sync.dma_start(out=b1_rows[0:CHUNKS, :], in_=b_m1.rearrange("(t p) -> t p", p=P))
         w_raw["w_e2"] = load_w1("w_e2", 2)
         load_e(0, pieces=2)
@@ -128,28 +127,22 @@ def tile_messagepassing_pa_t_kernel(tc, h, e, adj_mask, W_m1, b_m1, W_m2, b_m2, 
             in_=W_m2.rearrange("(t p) n -> p t n", p=P),
         )
         load_e(2)
-        load_h(1)
         for step in range(3, GROUPS - 2):
             load_e(step)
+        mask_wide = keep.tile([P, NODES * P // 2], F32, name="mask_wide")
 
         def spread_mask():
-            mask_t_ps = ps_m.tile([P, P], BF16, name="mask_t_ps", tag="mask")
+            mask_t_ps = ps_2.tile([P, P], BF16, name="mask_t_ps", tag="out_ps")
             nc.tensor.transpose(mask_t_ps[:], mask_in[:], ident_bf16[:])
             mask_t = keep.tile([P, P], BF16, name="mask_t")
             nc.scalar.copy(out=mask_t[:], in_=mask_t_ps[:])
-            words = NODES * P // 2
-            parked = out.rearrange("b i k -> (b i k)")[0 : HALVES * words]
+            parked = out.rearrange("b i k -> (b i k)")[0 : HALVES * NODES * P // 2]
             nc.sync.dma_start(
                 out=parked.rearrange("(r w) -> r w", w=P // 2), in_=mask_t[0 : HALVES * NODES, :].bitcast(F32)
             )
-            for step in range(GROUPS - 2, GROUPS):
+            for step in range(GROUPS - 2, steps):
                 load_e(step)
-            for half in range(HALVES):
-                wide = keep.tile([P, words], F32, name="mask_wide%d" % half)
-                nc.sync.dma_start(out=wide[:], in_=parked[half * words : (half + 1) * words].partition_broadcast(P))
-                mask_wide.append(wide)
-            for step in range(GROUPS, steps):
-                load_e(step)
+            nc.sync.dma_start(out=mask_wide[:], in_=parked[NODES * P // 2 :].partition_broadcast(P))
             nc.sync.dma_start(out=b2_all[:], in_=b_m2.partition_broadcast(P))
 
         weights = {}
@@ -168,25 +161,27 @@ def tile_messagepassing_pa_t_kernel(tc, h, e, adj_mask, W_m1, b_m1, W_m2, b_m2, 
             weights[name] = mx_operand(keep, H, name)
             quantise(nc, weights[name], w_grouped[name][:])
 
-        h_once, h_grouped, h_once_mx, h_mx = {}, {}, {}, {}
+        h_once = keep.tile([P, HALVES * P * 2], F32, name="h_once", align_bytes=64)
+        h_once_mx = mx_operand(keep, HALVES * P, "h_once_mx")
+        h_grouped, h_mx = {}, {}
 
-        def transpose_h(half):
-            h_words = h_sb[half][:].bitcast(F32)
-            h_ps = ps_t.tile([P, 2 * P], F32, name="h_ps", tag="transposed")
-            for u in range(2):
-                nc.tensor.transpose(h_ps[:, u * P : (u + 1) * P], h_words[:, u * P : (u + 1) * P], ident_f32[:])
-            once = keep.tile([P, 2 * P], F32, name="h_once%d" % half, align_bytes=64)
-            nc.scalar.copy(out=once[:].rearrange("p (c u) -> p c u", u=2), in_=h_ps[:].rearrange("p (u c) -> p c u", u=2))
-            grouped = keep.tile([P, J_GROUP * P * 2], F32, name="h_grouped%d" % half, align_bytes=64)
+        def transpose_h():
+            h_ps = ps_t.tile([P, HALVES * 2 * P], F32, name="h_ps", tag="transposed")
+            for block in range(HALVES * 2):
+                half, u = divmod(block, 2)
+                h_words = h_sb[half][:].bitcast(F32)
+                nc.tensor.transpose(h_ps[:, block * P : (block + 1) * P], h_words[:, u * P : (u + 1) * P], ident_f32[:])
             nc.scalar.copy(
-                out=grouped[:].rearrange("p (r w) -> p r w", r=J_GROUP),
-                in_=once[:].unsqueeze(1).to_broadcast([P, J_GROUP, 2 * P]),
+                out=h_once[:].rearrange("p (a c u) -> p a c u", a=HALVES, u=2),
+                in_=h_ps[:].rearrange("p (a u c) -> p a c u", a=HALVES, u=2),
             )
-            h_once[half], h_grouped[half] = once, grouped
 
-        def quantise_h_once(half):
-            h_once_mx[half] = mx_operand(keep, P, "h_once_mx%d" % half)
-            quantise(nc, h_once_mx[half], h_once[half][:].bitcast(BF16))
+        def repeat_h(half):
+            h_grouped[half] = keep.tile([P, J_GROUP * P * 2], F32, name="h_grouped%d" % half, align_bytes=64)
+            nc.scalar.copy(
+                out=h_grouped[half][:].rearrange("p (r w) -> p r w", r=J_GROUP),
+                in_=h_once[:, half * 2 * P : (half + 1) * 2 * P].unsqueeze(1).to_broadcast([P, J_GROUP, 2 * P]),
+            )
 
         def quantise_h(half):
             h_mx[half] = mx_operand(keep, COLS, "h_mx%d" % half)
@@ -195,17 +190,18 @@ def tile_messagepassing_pa_t_kernel(tc, h, e, adj_mask, W_m1, b_m1, W_m2, b_m2, 
         aj_b1 = keep.tile([P, CHUNKS * HALVES * P], F32, name="aj_b1")
         b1_pp = keep.tile([P, CHUNKS], F32, name="b1_pp")
 
-        def compute_aj(half, aj_ps):
+        def compute_aj():
+            banks = []
+            width = HALVES * P
             for t in range(CHUNKS):
-                mx_pass(
-                    nc, aj_ps[:, t * P : (t + 1) * P], weights["w_xj"], t * P, (h_once_mx[half][0][:], h_once_mx[half][1][:]), True, True
-                )
+                if t % 2 == 0:
+                    banks.append(ps_1.tile([P, 2 * width], F32, name="aj_ps", tag="stage1"))
+                part = banks[-1][:, t % 2 * width : (t % 2 + 1) * width]
+                mx_pass(nc, part, weights["w_xj"], t * P, (h_once_mx[0][:], h_once_mx[1][:]), True, True)
             for t in range(CHUNKS):
+                part = banks[t // 2][:, t % 2 * width : (t % 2 + 1) * width]
                 nc.scalar.activation(
-                    out=aj_b1[:, (t * HALVES + half) * P : (t * HALVES + half + 1) * P],
-                    in_=aj_ps[:, t * P : (t + 1) * P],
-                    func=ACT.Identity,
-                    bias=b1_pp[:, t : t + 1],
+                    out=aj_b1[:, t * width : (t + 1) * width], in_=part, func=ACT.Identity, bias=b1_pp[:, t : t + 1]
                 )
 
         base, diagonals = [], []
@@ -227,6 +223,7 @@ def tile_messagepassing_pa_t_kernel(tc, h, e, adj_mask, W_m1, b_m1, W_m2, b_m2, 
 
         e_grouped, e_mx, mask_cols, p_ps, pre, r_grouped, r_mx = {}, {}, {}, {}, {}, {}, {}
         out_ps = {}
+        sum_0 = keep.tile([P, H], F32, name="sum_0")
 
         def transpose_e(step):
             e_words = e_sb[step][:].bitcast(F32)
@@ -248,12 +245,12 @@ def tile_messagepassing_pa_t_kernel(tc, h, e, adj_mask, W_m1, b_m1, W_m2, b_m2, 
 
         def lay_out_mask(step):
             half, group = divmod(step, GROUPS)
-            if step >= STEPS_MASKED_BY_TENSOR:
-                mask_cols[step] = mask_wide[half][:].bitcast(BF16)[:, group * COLS : (group + 1) * COLS]
+            if half == 1:
+                mask_cols[step] = mask_wide[:].bitcast(BF16)[:, group * COLS : (group + 1) * COLS]
                 return
             mask_ps = ps_m.tile([P, COLS], BF16, name="mask_ps", tag="mask")
             for j in range(J_GROUP):
-                source = half * NODES + group * J_GROUP + j
+                source = group * J_GROUP + j
                 nc.tensor.matmul(
                     mask_ps[:, j * P : (j + 1) * P],
                     lhsT=mask_in[:, source : source + 1].to_broadcast([P, P]),
@@ -276,7 +273,7 @@ def tile_messagepassing_pa_t_kernel(tc, h, e, adj_mask, W_m1, b_m1, W_m2, b_m2, 
             p_ps[step] = banks
 
         def scalar_adds(step):
-            return step % 4 == 2
+            return step % 2 == (1 if step < GROUPS else 0) and step != GROUPS or step >= steps - 3
 
         def add_aj_on_scalar(step):
             half, group = divmod(step, GROUPS)
@@ -358,6 +355,8 @@ def tile_messagepassing_pa_t_kernel(tc, h, e, adj_mask, W_m1, b_m1, W_m2, b_m2, 
             if 0 <= s < steps - 1:
                 apply_mask(s, 0, COLS)
                 relu_on_scalar(s, 0, COLS)
+            if s == GROUPS + 1:
+                nc.scalar.copy(out=sum_0[:], in_=out_ps[0][:])
             if s + 3 < steps:
                 transpose_e(s + 3)
             elif s + 3 - steps in range(HALVES):
@@ -376,17 +375,18 @@ def tile_messagepassing_pa_t_kernel(tc, h, e, adj_mask, W_m1, b_m1, W_m2, b_m2, 
                 stage_2(s - 1, range(J_GROUP))
 
         regroup_weight("w_xj", nc.scalar.copy, 0, H // 2)
-        transpose_h(0)
+        transpose_h()
+        repeat_h(0)
         b1_ps = ps_t.tile([P, P], BF16, name="b1_ps", tag="transposed")
         nc.tensor.transpose(b1_ps[:], b1_rows[:], ident_bf16[:])
         regroup_weight("w_xj", nc.vector.tensor_copy, H // 2, H // 2)
         quantise_weight("w_xj")
-        quantise_h_once(0)
+        quantise(nc, h_once_mx, h_once[:].bitcast(BF16))
         nc.vector.tensor_copy(out=b1_pp[:], in_=b1_ps[:, 0:CHUNKS])
         regroup_weight("w_e2", nc.vector.tensor_copy)
         pipeline_step(-3)
         regroup_weight("w_xi", nc.scalar.copy, 0, H // 2)
-        compute_aj(0, ps_1.tile([P, CHUNKS * P], F32, name="aj_ps0", tag="stage1"))
+        compute_aj()
         quantise_h(0)
         quantise_weight("w_e2")
         regroup_weight("w_xi", nc.vector.tensor_copy, H // 2, H // 2)
@@ -396,8 +396,6 @@ def tile_messagepassing_pa_t_kernel(tc, h, e, adj_mask, W_m1, b_m1, W_m2, b_m2, 
         pipeline_step(-2)
         regroup_weight("w_m2", nc.scalar.copy)
         pipeline_step(-1)
-
-        sum_0 = keep.tile([P, H], F32, name="sum_0")
 
         def store_result(half, total, pieces):
             width = H // pieces
@@ -411,16 +409,12 @@ def tile_messagepassing_pa_t_kernel(tc, h, e, adj_mask, W_m1, b_m1, W_m2, b_m2, 
             pipeline_step(s)
             if s == 0:
                 quantise_weight("w_m2")
-            if s == 2:
-                transpose_h(1)
             if s == GROUPS + 1:
                 for half in range(HALVES):
                     compute_diagonal(half)
-            if s == GROUPS:
-                nc.scalar.copy(out=sum_0[:], in_=out_ps[0][:])
-            if s == 4:
-                quantise_h_once(1)
-                compute_aj(1, ps_t.tile([P, CHUNKS * P], F32, name="aj_ps1", tag="transposed"))
+            if s == 3:
+                repeat_h(1)
+            if s == 5:
                 quantise_h(1)
 
         last = steps - 1

@@ -23,6 +23,8 @@ J_GROUP = 4
 GROUPS = NODES // J_GROUP
 COLS = J_GROUP * P
 LAST_J = J_GROUP - 1
+STEPS_MASKED_BY_TENSOR = 5
+SCALAR_SHARE = 3 * H // 8
 
 FLOPS = 2 * (2 * GRAPHS * NODES * H * H + 2 * GRAPHS * NODES * NODES * H * H)
 
@@ -129,7 +131,10 @@ def tile_messagepassing_pa_t_kernel(tc, h, e, adj_mask, W_m1, b_m1, W_m2, b_m2, 
         load_e(2)
         for step in range(3, GROUPS - 2):
             load_e(step)
-        mask_wide = keep.tile([P, NODES * P // 2], F32, name="mask_wide")
+        wide_steps = HALVES * GROUPS - STEPS_MASKED_BY_TENSOR
+        mask_wide = keep.tile([P, wide_steps * COLS // 2], F32, name="mask_wide")
+
+        nc.sync.dma_start(out=b2_all[:], in_=b_m2.partition_broadcast(P))
 
         def spread_mask():
             mask_t_ps = ps_2.tile([P, P], BF16, name="mask_t_ps", tag="out_ps")
@@ -140,10 +145,14 @@ def tile_messagepassing_pa_t_kernel(tc, h, e, adj_mask, W_m1, b_m1, W_m2, b_m2, 
             nc.sync.dma_start(
                 out=parked.rearrange("(r w) -> r w", w=P // 2), in_=mask_t[0 : HALVES * NODES, :].bitcast(F32)
             )
-            for step in range(GROUPS - 2, steps):
+            skipped = STEPS_MASKED_BY_TENSOR * COLS // 2
+            half_1 = GROUPS * COLS // 2
+            for step in range(GROUPS - 2, GROUPS + 2):
                 load_e(step)
-            nc.sync.dma_start(out=mask_wide[:], in_=parked[NODES * P // 2 :].partition_broadcast(P))
-            nc.sync.dma_start(out=b2_all[:], in_=b_m2.partition_broadcast(P))
+            nc.sync.dma_start(out=mask_wide[:, 0 : half_1 - skipped], in_=parked[skipped:half_1].partition_broadcast(P))
+            for step in range(GROUPS + 2, steps):
+                load_e(step)
+            nc.sync.dma_start(out=mask_wide[:, half_1 - skipped :], in_=parked[half_1:].partition_broadcast(P))
 
         weights = {}
         w_grouped = {}
@@ -213,8 +222,7 @@ def tile_messagepassing_pa_t_kernel(tc, h, e, adj_mask, W_m1, b_m1, W_m2, b_m2, 
             nc.scalar.activation(out=diagonal[:], in_=ident_bf16[:], func=ACT.Copy, scale=degree[:, 0:1])
             diagonals.append(diagonal)
 
-        def compute_base(half):
-            base_ps = ps_t.tile([P, H], F32, name="base_ps", tag="transposed")
+        def compute_base(half, base_ps):
             nc.tensor.matmul(base_ps[:], lhsT=ident_bf16[:], rhs=h_sb[half][:], start=True, stop=False)
             nc.tensor.matmul(base_ps[:], lhsT=diagonals[half][:], rhs=b2_all[:], start=False, stop=True)
             rows_base = keep.tile([P, H], F32, name="base%d" % half)
@@ -245,8 +253,9 @@ def tile_messagepassing_pa_t_kernel(tc, h, e, adj_mask, W_m1, b_m1, W_m2, b_m2, 
 
         def lay_out_mask(step):
             half, group = divmod(step, GROUPS)
-            if half == 1:
-                mask_cols[step] = mask_wide[:].bitcast(BF16)[:, group * COLS : (group + 1) * COLS]
+            if step >= STEPS_MASKED_BY_TENSOR:
+                wide_step = step - STEPS_MASKED_BY_TENSOR
+                mask_cols[step] = mask_wide[:].bitcast(BF16)[:, wide_step * COLS : (wide_step + 1) * COLS]
                 return
             mask_ps = ps_m.tile([P, COLS], BF16, name="mask_ps", tag="mask")
             for j in range(J_GROUP):
@@ -352,17 +361,19 @@ def tile_messagepassing_pa_t_kernel(tc, h, e, adj_mask, W_m1, b_m1, W_m2, b_m2, 
         def pipeline_step(s):
             if 0 <= s + 1 < steps:
                 add_aj_on_scalar(s + 1)
-            if 0 <= s < steps - 1:
+            if 0 <= s:
                 apply_mask(s, 0, COLS)
                 relu_on_scalar(s, 0, COLS)
             if s == GROUPS + 1:
                 nc.scalar.copy(out=sum_0[:], in_=out_ps[0][:])
             if s + 3 < steps:
                 transpose_e(s + 3)
-            elif s + 3 - steps in range(HALVES):
-                compute_base(s + 3 - steps)
+            elif s == steps - 3:
+                compute_base(1, ps_t.tile([P, H], F32, name="base_ps1", tag="transposed"))
             if 0 <= s + 2 < steps:
                 lay_out_mask(s + 2)
+            if s == 0:
+                compute_base(0, ps_2.tile([P, H], F32, name="base_ps0", tag="out_ps"))
             if 0 <= s + 1 < steps:
                 add_aj(s + 1)
             if s + 2 == 0:
@@ -374,12 +385,12 @@ def tile_messagepassing_pa_t_kernel(tc, h, e, adj_mask, W_m1, b_m1, W_m2, b_m2, 
                 quantise_r(s - 1, 0, COLS)
                 stage_2(s - 1, range(J_GROUP))
 
-        regroup_weight("w_xj", nc.scalar.copy, 0, H // 2)
+        regroup_weight("w_xj", nc.scalar.copy, 0, SCALAR_SHARE)
         transpose_h()
         repeat_h(0)
         b1_ps = ps_t.tile([P, P], BF16, name="b1_ps", tag="transposed")
         nc.tensor.transpose(b1_ps[:], b1_rows[:], ident_bf16[:])
-        regroup_weight("w_xj", nc.vector.tensor_copy, H // 2, H // 2)
+        regroup_weight("w_xj", nc.vector.tensor_copy, SCALAR_SHARE, H - SCALAR_SHARE)
         quantise_weight("w_xj")
         quantise(nc, h_once_mx, h_once[:].bitcast(BF16))
         nc.vector.tensor_copy(out=b1_pp[:], in_=b1_ps[:, 0:CHUNKS])
@@ -396,6 +407,8 @@ def tile_messagepassing_pa_t_kernel(tc, h, e, adj_mask, W_m1, b_m1, W_m2, b_m2, 
         pipeline_step(-2)
         regroup_weight("w_m2", nc.scalar.copy)
         pipeline_step(-1)
+        for half in range(HALVES):
+            compute_diagonal(half)
 
         def store_result(half, total, pieces):
             width = H // pieces
@@ -405,29 +418,35 @@ def tile_messagepassing_pa_t_kernel(tc, h, e, adj_mask, W_m1, b_m1, W_m2, b_m2, 
                 nc.vector.tensor_tensor(out=result[:], in0=total[:, part], in1=base[half][:, part], op=ALU.add)
                 nc.sync.dma_start(out=out_rows[half * P : (half + 1) * P, part], in_=result[:])
 
-        for s in range(steps - 1):
+        for s in range(steps - 2):
             pipeline_step(s)
             if s == 0:
                 quantise_weight("w_m2")
-            if s == GROUPS + 1:
-                for half in range(HALVES):
-                    compute_diagonal(half)
             if s == 3:
                 repeat_h(1)
             if s == 5:
                 quantise_h(1)
 
         last = steps - 1
-        apply_mask(last, COLS // 2, COLS // 2)
-        for j in (2, LAST_J):
-            relu_on_scalar(last, j * P, P)
-        apply_mask(last, 0, COLS // 2)
-        quantise_r(last - 1, 0, COLS)
-        stage_2(last - 1, range(J_GROUP))
-        relu_on_vector(last, 0, COLS // 2)
-        quantise_r(last, 0, COLS // 2)
-        stage_2(last, (0, 1))
-        for j in (2, LAST_J):
+        pair = COLS // 2
+        add_aj_on_scalar(last)
+        for first in (0, pair):
+            apply_mask(last - 1, first, pair)
+            relu_on_scalar(last - 1, first, pair)
+        quantise_r(last - 2, 0, COLS)
+        stage_2(last - 2, range(J_GROUP))
+        add_aj(last)
+        quantise_r(last - 1, 0, pair)
+        stage_2(last - 1, (0, 1))
+        apply_mask(last, 0, pair)
+        relu_on_scalar(last, 0, P)
+        relu_on_scalar(last, P, P)
+        quantise_r(last - 1, pair, pair)
+        stage_2(last - 1, (2, 3))
+        apply_mask(last, pair, pair)
+        relu_on_scalar(last, LAST_J * P, P)
+        relu_on_vector(last, 2 * P, P)
+        for j in range(J_GROUP):
             quantise_r(last, j * P, P)
             stage_2(last, (j,))
         store_result(0, sum_0, 1)

@@ -282,7 +282,7 @@ def tile_messagepassing_pa_t_kernel(tc, h, e, adj_mask, W_m1, b_m1, W_m2, b_m2, 
             p_ps[step] = banks
 
         def scalar_adds(step):
-            return step % 2 == (1 if step < GROUPS else 0) and step != GROUPS or step >= steps - 3
+            return step > 0
 
         def add_aj_on_scalar(step):
             half, group = divmod(step, GROUPS)
@@ -332,6 +332,18 @@ def tile_messagepassing_pa_t_kernel(tc, h, e, adj_mask, W_m1, b_m1, W_m2, b_m2, 
             out_view, in_view = regrouping(step, first, width)
             nc.scalar.activation(out=out_view, in_=in_view, func=ACT.Relu)
 
+        def relu_on_gpsimd(step, first, width):
+            if step not in r_grouped:
+                r_grouped[step] = work.tile([P, COLS * PACK], BF16, name="r_grouped", align_bytes=64)
+            nc.gpsimd.tensor_scalar(
+                out=r_grouped[step][:, first * PACK : (first + width) * PACK].rearrange("p (c t) -> p c t", t=PACK),
+                in0=pre[step][:].rearrange("p (t c) -> p c t", t=PACK)[:, first : first + width, :],
+                scalar1=0.0,
+                scalar2=1.0,
+                op0=ALU.max,
+                op1=ALU.mult,
+            )
+
         def relu_on_vector(step, first, width):
             out_view, in_view = regrouping(step, first, width)
             nc.vector.tensor_scalar_max(out_view, in_view, 0.0)
@@ -363,7 +375,8 @@ def tile_messagepassing_pa_t_kernel(tc, h, e, adj_mask, W_m1, b_m1, W_m2, b_m2, 
                 add_aj_on_scalar(s + 1)
             if 0 <= s:
                 apply_mask(s, 0, COLS)
-                relu_on_scalar(s, 0, COLS)
+                relu_on_gpsimd(s, LAST_J * P, P)
+                relu_on_scalar(s, 0, LAST_J * P)
             if s == GROUPS + 1:
                 nc.scalar.copy(out=sum_0[:], in_=out_ps[0][:])
             if s + 3 < steps:

@@ -7,6 +7,7 @@ F32 = mybir.dt.float32
 BF16 = mybir.dt.bfloat16
 U32 = mybir.dt.uint32
 U8 = mybir.dt.uint8
+I32 = mybir.dt.int32
 FP8X4 = mybir.dt.float8_e4m3fn_x4
 ACT = mybir.ActivationFunctionType
 ALU = mybir.AluOpType
@@ -172,6 +173,7 @@ def tile_messagepassing_pa_t_kernel(tc, h, e, adj_mask, W_m1, b_m1, W_m2, b_m2, 
 
         h_once = keep.tile([P, HALVES * P * 2], F32, name="h_once", align_bytes=64)
         h_once_mx = mx_operand(keep, HALVES * P, "h_once_mx")
+        nc.gpsimd.memset(h_once_mx[1][:].bitcast(I32), 0)
         h_grouped, h_mx = {}, {}
 
         def transpose_h():
@@ -191,6 +193,16 @@ def tile_messagepassing_pa_t_kernel(tc, h, e, adj_mask, W_m1, b_m1, W_m2, b_m2, 
                 out=h_grouped[half][:].rearrange("p (r w) -> p r w", r=J_GROUP),
                 in_=h_once[:, half * 2 * P : (half + 1) * 2 * P].unsqueeze(1).to_broadcast([P, J_GROUP, 2 * P]),
             )
+
+        def repeat_h_codes(half):
+            h_mx[half] = mx_operand(keep, COLS, "h_mx%d" % half)
+            for once, wide in zip(h_once_mx, h_mx[half]):
+                words_once = once[:].bitcast(I32)
+                width = words_once.shape[1] // HALVES
+                nc.sync.dma_start(
+                    out=wide[:].bitcast(I32).rearrange("p (r c) -> p r c", r=J_GROUP),
+                    in_=words_once[:, half * width : (half + 1) * width].unsqueeze(1).to_broadcast([P, J_GROUP, width]),
+                )
 
         def quantise_h(half):
             h_mx[half] = mx_operand(keep, COLS, "h_mx%d" % half)
@@ -217,7 +229,10 @@ def tile_messagepassing_pa_t_kernel(tc, h, e, adj_mask, W_m1, b_m1, W_m2, b_m2, 
 
         def compute_diagonal(half):
             degree = keep.tile([P, 1], F32, name="degree%d" % half)
-            nc.vector.reduce_sum(out=degree[:], in_=mask_in[:, half * NODES : (half + 1) * NODES], axis=mybir.AxisListType.X)
+            counted = keep.tile([P, NODES], BF16, name="counted%d" % half)
+            nc.scalar.activation(
+                out=counted[:], in_=mask_in[:, half * NODES : (half + 1) * NODES], func=ACT.Copy, accum_out=degree[:]
+            )
             diagonal = keep.tile([P, P], BF16, name="diagonal%d" % half)
             nc.scalar.activation(out=diagonal[:], in_=ident_bf16[:], func=ACT.Copy, scale=degree[:, 0:1])
             diagonals.append(diagonal)
@@ -231,7 +246,6 @@ def tile_messagepassing_pa_t_kernel(tc, h, e, adj_mask, W_m1, b_m1, W_m2, b_m2, 
 
         e_grouped, e_mx, mask_cols, p_ps, pre, r_grouped, r_mx = {}, {}, {}, {}, {}, {}, {}
         out_ps = {}
-        sum_0 = keep.tile([P, H], F32, name="sum_0")
 
         def transpose_e(step):
             e_words = e_sb[step][:].bitcast(F32)
@@ -281,30 +295,28 @@ def tile_messagepassing_pa_t_kernel(tc, h, e, adj_mask, W_m1, b_m1, W_m2, b_m2, 
                 banks.append(bank)
             p_ps[step] = banks
 
-        def scalar_adds(step):
-            return step > 0
+        def scalar_chunks(step):
+            return 0 if step < 2 else 2 if step == steps - 2 else 1
 
         def add_aj_on_scalar(step):
             half, group = divmod(step, GROUPS)
             pre[step] = work.tile([P, CHUNKS * COLS], BF16, name="pre")
-            if not scalar_adds(step):
-                return
-            t = 0
-            for j in range(J_GROUP):
-                for b in range(GRAPHS_PER_HALF):
-                    run = slice((j * GRAPHS_PER_HALF + b) * NODES, (j * GRAPHS_PER_HALF + b + 1) * NODES)
-                    source = (t * HALVES + half) * P + b * NODES + group * J_GROUP + j
-                    nc.scalar.activation(
-                        out=pre[step][:, t * COLS : (t + 1) * COLS][:, run],
-                        in_=p_ps[step][t][:, run],
-                        func=ACT.Identity,
-                        bias=aj_b1[:, source : source + 1],
-                    )
+            for t in range(scalar_chunks(step)):
+                for j in range(J_GROUP):
+                    for b in range(GRAPHS_PER_HALF):
+                        run = slice((j * GRAPHS_PER_HALF + b) * NODES, (j * GRAPHS_PER_HALF + b + 1) * NODES)
+                        source = (t * HALVES + half) * P + b * NODES + group * J_GROUP + j
+                        nc.scalar.activation(
+                            out=pre[step][:, t * COLS : (t + 1) * COLS][:, run],
+                            in_=p_ps[step][t][:, run],
+                            func=ACT.Identity,
+                            bias=aj_b1[:, source : source + 1],
+                        )
 
         def add_aj(step):
             half, group = divmod(step, GROUPS)
             tile_pre = pre[step]
-            for t in range(1 if scalar_adds(step) else 0, CHUNKS):
+            for t in range(scalar_chunks(step), CHUNKS):
                 aj = aj_b1[:, (t * HALVES + half) * P : (t * HALVES + half + 1) * P]
                 nc.vector.tensor_tensor(
                     out=tile_pre[:, t * COLS : (t + 1) * COLS].rearrange("p (j b i) -> p j b i", j=J_GROUP, b=GRAPHS_PER_HALF),
@@ -358,7 +370,7 @@ def tile_messagepassing_pa_t_kernel(tc, h, e, adj_mask, W_m1, b_m1, W_m2, b_m2, 
         def stage_2(step, js):
             half, group = divmod(step, GROUPS)
             if half not in out_ps:
-                out_ps[half] = ps_2.tile([P, H], F32, name="out_ps%d" % half, tag="out_ps")
+                out_ps[half] = (ps_2, ps_m)[half].tile([P, H], F32, name="out_ps%d" % half, tag=("out_ps", "mask")[half])
             for j in js:
                 mx_pass(
                     nc,
@@ -377,8 +389,6 @@ def tile_messagepassing_pa_t_kernel(tc, h, e, adj_mask, W_m1, b_m1, W_m2, b_m2, 
                 apply_mask(s, 0, COLS)
                 relu_on_gpsimd(s, LAST_J * P, P)
                 relu_on_scalar(s, 0, LAST_J * P)
-            if s == GROUPS + 1:
-                nc.scalar.copy(out=sum_0[:], in_=out_ps[0][:])
             if s + 3 < steps:
                 transpose_e(s + 3)
             elif s == steps - 3:
@@ -387,12 +397,13 @@ def tile_messagepassing_pa_t_kernel(tc, h, e, adj_mask, W_m1, b_m1, W_m2, b_m2, 
                 lay_out_mask(s + 2)
             if s == 0:
                 compute_base(0, ps_2.tile([P, H], F32, name="base_ps0", tag="out_ps"))
+            if 0 < s + 2 < steps:
+                quantise_e(s + 2)
             if 0 <= s + 1 < steps:
                 add_aj(s + 1)
             if s + 2 == 0:
                 stage_1(0)
             elif 0 < s + 2 < steps:
-                quantise_e(s + 2)
                 stage_1(s + 2)
             if 0 <= s - 1:
                 quantise_r(s - 1, 0, COLS)
@@ -417,8 +428,9 @@ def tile_messagepassing_pa_t_kernel(tc, h, e, adj_mask, W_m1, b_m1, W_m2, b_m2, 
         quantise_e(0)
         quantise_weight("w_xi")
         spread_mask()
+        repeat_h_codes(1)
         pipeline_step(-2)
-        regroup_weight("w_m2", nc.scalar.copy)
+        regroup_weight("w_m2", nc.scalar.copy, 0 * H // 16, 16 * H // 16)
         pipeline_step(-1)
         for half in range(HALVES):
             compute_diagonal(half)
@@ -435,10 +447,6 @@ def tile_messagepassing_pa_t_kernel(tc, h, e, adj_mask, W_m1, b_m1, W_m2, b_m2, 
             pipeline_step(s)
             if s == 0:
                 quantise_weight("w_m2")
-            if s == 3:
-                repeat_h(1)
-            if s == 5:
-                quantise_h(1)
 
         last = steps - 1
         pair = COLS // 2
@@ -462,5 +470,5 @@ def tile_messagepassing_pa_t_kernel(tc, h, e, adj_mask, W_m1, b_m1, W_m2, b_m2, 
         for j in range(J_GROUP):
             quantise_r(last, j * P, P)
             stage_2(last, (j,))
-        store_result(0, sum_0, 1)
+        store_result(0, out_ps[0], 1)
         store_result(1, out_ps[1], 2)

@@ -24,7 +24,7 @@ J_GROUP = 4
 GROUPS = NODES // J_GROUP
 COLS = J_GROUP * P
 LAST_J = J_GROUP - 1
-STEPS_MASKED_BY_TENSOR = 5
+STEPS_MASKED_BY_TENSOR = 4
 SCALAR_SHARE = 3 * H // 8
 
 FLOPS = 2 * (2 * GRAPHS * NODES * H * H + 2 * GRAPHS * NODES * NODES * H * H)
@@ -412,7 +412,7 @@ def tile_messagepassing_pa_t_kernel(tc, h, e, adj_mask, W_m1, b_m1, W_m2, b_m2, 
         regroup_weight("w_xj", nc.scalar.copy, 0, SCALAR_SHARE)
         transpose_h()
         repeat_h(0)
-        b1_ps = ps_t.tile([P, P], BF16, name="b1_ps", tag="transposed")
+        b1_ps = ps_2.tile([P, P], BF16, name="b1_ps", tag="out_ps")
         nc.tensor.transpose(b1_ps[:], b1_rows[:], ident_bf16[:])
         regroup_weight("w_xj", nc.vector.tensor_copy, SCALAR_SHARE, H - SCALAR_SHARE)
         quantise_weight("w_xj")
@@ -420,11 +420,11 @@ def tile_messagepassing_pa_t_kernel(tc, h, e, adj_mask, W_m1, b_m1, W_m2, b_m2, 
         nc.vector.tensor_copy(out=b1_pp[:], in_=b1_ps[:, 0:CHUNKS])
         regroup_weight("w_e2", nc.vector.tensor_copy)
         pipeline_step(-3)
-        regroup_weight("w_xi", nc.scalar.copy, 0, H // 2)
+        regroup_weight("w_xi", nc.scalar.copy, 0, 4 * H // 16)
         compute_aj()
         quantise_h(0)
         quantise_weight("w_e2")
-        regroup_weight("w_xi", nc.vector.tensor_copy, H // 2, H // 2)
+        regroup_weight("w_xi", nc.vector.tensor_copy, 4 * H // 16, H - 4 * H // 16)
         quantise_e(0)
         quantise_weight("w_xi")
         spread_mask()

@@ -225,23 +225,21 @@ def tile_messagepassing_pa_t_kernel(tc, h, e, adj_mask, W_m1, b_m1, W_m2, b_m2, 
                     out=aj_b1[:, t * width : (t + 1) * width], in_=part, func=ACT.Identity, bias=b1_pp[:, t : t + 1]
                 )
 
-        base, diagonals = [], []
+        base, degrees = [], []
 
-        def compute_diagonal(half):
+        def compute_degree(half):
             degree = keep.tile([P, 1], F32, name="degree%d" % half)
+            degrees.append(degree)
             counted = keep.tile([P, NODES], BF16, name="counted%d" % half)
             nc.scalar.activation(
                 out=counted[:], in_=mask_in[:, half * NODES : (half + 1) * NODES], func=ACT.Copy, accum_out=degree[:]
             )
-            diagonal = keep.tile([P, P], BF16, name="diagonal%d" % half)
-            nc.scalar.activation(out=diagonal[:], in_=ident_bf16[:], func=ACT.Copy, scale=degree[:, 0:1])
-            diagonals.append(diagonal)
 
-        def compute_base(half, base_ps):
-            nc.tensor.matmul(base_ps[:], lhsT=ident_bf16[:], rhs=h_sb[half][:], start=True, stop=False)
-            nc.tensor.matmul(base_ps[:], lhsT=diagonals[half][:], rhs=b2_all[:], start=False, stop=True)
+        def compute_base(half):
             rows_base = keep.tile([P, H], F32, name="base%d" % half)
-            nc.scalar.copy(out=rows_base[:], in_=base_ps[:])
+            nc.vector.scalar_tensor_tensor(
+                out=rows_base[:], in0=b2_all[:], scalar=degrees[half][:, 0:1], in1=h_sb[half][:], op0=ALU.mult, op1=ALU.add
+            )
             base.append(rows_base)
 
         e_grouped, e_mx, mask_cols, p_ps, pre, r_grouped, r_mx = {}, {}, {}, {}, {}, {}, {}
@@ -296,7 +294,7 @@ def tile_messagepassing_pa_t_kernel(tc, h, e, adj_mask, W_m1, b_m1, W_m2, b_m2, 
             p_ps[step] = banks
 
         def scalar_chunks(step):
-            return 0 if step < 2 else 2 if step == steps - 2 else 1
+            return 0 if step == 0 else 2 if step == steps - 2 else 1
 
         def add_aj_on_scalar(step):
             half, group = divmod(step, GROUPS)
@@ -387,16 +385,18 @@ def tile_messagepassing_pa_t_kernel(tc, h, e, adj_mask, W_m1, b_m1, W_m2, b_m2, 
                 add_aj_on_scalar(s + 1)
             if 0 <= s:
                 apply_mask(s, 0, COLS)
-                relu_on_gpsimd(s, LAST_J * P, P)
-                relu_on_scalar(s, 0, LAST_J * P)
+                if s + 3 < steps:
+                    relu_on_gpsimd(s, LAST_J * P, P)
+                    relu_on_scalar(s, 0, LAST_J * P)
+                else:
+                    relu_on_scalar(s, 0, COLS)
+            if s == steps - 3:
+                for half in range(HALVES):
+                    compute_base(half)
             if s + 3 < steps:
                 transpose_e(s + 3)
-            elif s == steps - 3:
-                compute_base(1, ps_t.tile([P, H], F32, name="base_ps1", tag="transposed"))
             if 0 <= s + 2 < steps:
                 lay_out_mask(s + 2)
-            if s == 0:
-                compute_base(0, ps_2.tile([P, H], F32, name="base_ps0", tag="out_ps"))
             if 0 < s + 2 < steps:
                 quantise_e(s + 2)
             if 0 <= s + 1 < steps:
@@ -433,7 +433,7 @@ def tile_messagepassing_pa_t_kernel(tc, h, e, adj_mask, W_m1, b_m1, W_m2, b_m2, 
         regroup_weight("w_m2", nc.scalar.copy, 0 * H // 16, 16 * H // 16)
         pipeline_step(-1)
         for half in range(HALVES):
-            compute_diagonal(half)
+            compute_degree(half)
 
         def store_result(half, total, pieces):
             width = H // pieces

from contextlib import ExitStack

import concourse.mybir as mybir
from concourse.masks import make_identity

F32 = mybir.dt.float32
BF16 = mybir.dt.bfloat16
U32 = mybir.dt.uint32
U8 = mybir.dt.uint8
I32 = mybir.dt.int32
FP8X4 = mybir.dt.float8_e4m3fn_x4
ACT = mybir.ActivationFunctionType
ALU = mybir.AluOpType

P = 128
PACK = 4
GRAPHS = 8
NODES = 32
H = 512
CHUNKS = H // P
HALVES = 2
GRAPHS_PER_HALF = GRAPHS // HALVES
J_GROUP = 4
GROUPS = NODES // J_GROUP
COLS = J_GROUP * P
LAST_J = J_GROUP - 1
STEPS_MASKED_BY_TENSOR = 4
SCALAR_SHARE = 3 * H // 8

FLOPS = 2 * (2 * GRAPHS * NODES * H * H + 2 * GRAPHS * NODES * NODES * H * H)


def quantise(nc, operand, values):
    codes, scales = operand
    nc.vector.quantize_mx(out=codes.bitcast(FP8X4), scales=scales, in_=values)


def mx_operand(pool, width, name):
    codes = pool.tile([P, width], U32, name=name + "_codes", align_bytes=64)
    scales = pool.tile([P, width], U8, name=name + "_scales", align_bytes=64)
    return codes, scales


def mx_pass(nc, acc, stationary, first, moving, start, stop):
    nc.tensor.matmul_mx(
        out=acc,
        lhsT=stationary[0][:, first : first + P].bitcast(FP8X4),
        lhsT_scale=stationary[1][:, first : first + P],
        rhs=moving[0].bitcast(FP8X4),
        rhs_scale=moving[1],
        start=start,
        stop=stop,
    )


def tile_messagepassing_pa_t_kernel(tc, h, e, adj_mask, W_m1, b_m1, W_m2, b_m2, out):
    nc = tc.nc
    h_rows = h.flatten_outer_dims()
    e_rows = e.rearrange("b i j k -> (b i) (j k)")
    mask_by_row = adj_mask.rearrange("b i j o -> (b i) (j o)")
    out_rows = out.flatten_outer_dims()
    steps = HALVES * GROUPS

    with ExitStack() as ctx:
        keep = ctx.enter_context(tc.tile_pool(name="keep", bufs=1))
        wstage = ctx.enter_context(tc.tile_pool(name="wstage", bufs=2))
        e_pool = ctx.enter_context(tc.tile_pool(name="e_pool", bufs=16))
        work = ctx.enter_context(tc.tile_pool(name="work", bufs=3))
        ps_t = ctx.enter_context(tc.psum_pool(name="ps_t", bufs=2))
        ps_1 = ctx.enter_context(tc.psum_pool(name="ps_1", bufs=4))
        ps_2 = ctx.enter_context(tc.psum_pool(name="ps_2", bufs=1))
        ps_m = ctx.enter_context(tc.psum_pool(name="ps_m", bufs=1))
        ctx.enter_context(tc.manual_schedule())

        ident_f32 = keep.tile([P, P], F32, name="ident_f32")
        make_identity(nc, ident_f32[:])
        ident_bf16 = keep.tile([P, P], BF16, name="ident_bf16")
        make_identity(nc, ident_bf16[:])

        e_sb = {}

        def load_e(step, pieces=1):
            half, group = divmod(step, GROUPS)
            tile_e = e_pool.tile([P, J_GROUP * H], BF16, name="e_sb")
            width = J_GROUP * H // pieces
            for piece in range(pieces):
                first = group * J_GROUP * H + piece * width
                nc.sync.dma_start(
                    out=tile_e[:, piece * width : (piece + 1) * width],
                    in_=e_rows[half * P : (half + 1) * P, first : first + width],
                )
            e_sb[step] = tile_e

        def load_w1(name, block):
            raw = keep.tile([P, PACK * H], BF16, name=name + "_raw")
            nc.sync.dma_start(
                out=raw[:].rearrange("q (u f) -> q u f", u=2),
                in_=W_m1[block * H : (block + 1) * H, :].rearrange("(u q s) n -> q u (s n)", u=2, q=P, s=2),
            )
            return raw

        b1_rows = keep.tile([P, P], BF16, name="b1_rows")
        nc.vector.memset(b1_rows[:], 0.0)
        b2_all = keep.tile([P, H], BF16, name="b2_all")
        w_raw = {}
        mask_in = keep.tile([P, P], BF16, name="mask_in")
        nc.vector.memset(mask_in[:], 0.0)
        h_sb = []

        def load_h(half):
            h_tile = keep.tile([P, H], BF16, name="h_sb%d" % half)
            nc.sync.dma_start(out=h_tile[:], in_=h_rows[half * P : (half + 1) * P, :])
            h_sb.append(h_tile)

        w_raw["w_xj"] = load_w1("w_xj", 1)
        for half in range(HALVES):
            load_h(half)
        nc.sync.dma_start(out=b1_rows[0:CHUNKS, :], in_=b_m1.rearrange("(t p) -> t p", p=P))
        w_raw["w_e2"] = load_w1("w_e2", 2)
        load_e(0, pieces=2)
        w_raw["w_xi"] = load_w1("w_xi", 0)
        for half in range(HALVES):
            nc.sync.dma_start(
                out=mask_in[:, half * NODES : (half + 1) * NODES], in_=mask_by_row[half * P : (half + 1) * P, :]
            )
        load_e(1)
        w_raw["w_m2"] = keep.tile([P, PACK * H], BF16, name="w_m2_raw")
        nc.sync.dma_start(
            out=w_raw["w_m2"][:].rearrange("p (t n) -> p t n", t=PACK),
            in_=W_m2.rearrange("(t p) n -> p t n", p=P),
        )
        load_e(2)
        for step in range(3, GROUPS - 2):
            load_e(step)
        wide_steps = HALVES * GROUPS - STEPS_MASKED_BY_TENSOR
        mask_wide = keep.tile([P, wide_steps * COLS // 2], F32, name="mask_wide")

        nc.sync.dma_start(out=b2_all[:], in_=b_m2.partition_broadcast(P))

        def spread_mask():
            mask_t_ps = ps_2.tile([P, P], BF16, name="mask_t_ps", tag="out_ps")
            nc.tensor.transpose(mask_t_ps[:], mask_in[:], ident_bf16[:])
            mask_t = keep.tile([P, P], BF16, name="mask_t")
            nc.scalar.copy(out=mask_t[:], in_=mask_t_ps[:])
            parked = out.rearrange("b i k -> (b i k)")[0 : HALVES * NODES * P // 2]
            nc.sync.dma_start(
                out=parked.rearrange("(r w) -> r w", w=P // 2), in_=mask_t[0 : HALVES * NODES, :].bitcast(F32)
            )
            skipped = STEPS_MASKED_BY_TENSOR * COLS // 2
            half_1 = GROUPS * COLS // 2
            for step in range(GROUPS - 2, GROUPS + 2):
                load_e(step)
            nc.sync.dma_start(out=mask_wide[:, 0 : half_1 - skipped], in_=parked[skipped:half_1].partition_broadcast(P))
            for step in range(GROUPS + 2, steps):
                load_e(step)
            nc.sync.dma_start(out=mask_wide[:, half_1 - skipped :], in_=parked[half_1:].partition_broadcast(P))

        weights = {}
        w_grouped = {}

        def regroup_weight(name, engine_copy, first=0, width=H):
            if name not in w_grouped:
                w_grouped[name] = wstage.tile([P, H * PACK], BF16, name="w_grouped", align_bytes=64)
            columns = slice(first // 4, (first + width) // 4)
            engine_copy(
                out=w_grouped[name][:].rearrange("q (c i t) -> q c t i", i=4, t=PACK)[:, columns, :, :],
                in_=w_raw[name][:].rearrange("q (t c i) -> q c t i", t=PACK, i=4)[:, columns, :, :],
            )

        def quantise_weight(name):
            weights[name] = mx_operand(keep, H, name)
            quantise(nc, weights[name], w_grouped[name][:])

        h_once = keep.tile([P, HALVES * P * 2], F32, name="h_once", align_bytes=64)
        h_once_mx = mx_operand(keep, HALVES * P, "h_once_mx")
        nc.gpsimd.memset(h_once_mx[1][:].bitcast(I32), 0)
        h_grouped, h_mx = {}, {}

        def transpose_h():
            h_ps = ps_t.tile([P, HALVES * 2 * P], F32, name="h_ps", tag="transposed")
            for block in range(HALVES * 2):
                half, u = divmod(block, 2)
                h_words = h_sb[half][:].bitcast(F32)
                nc.tensor.transpose(h_ps[:, block * P : (block + 1) * P], h_words[:, u * P : (u + 1) * P], ident_f32[:])
            nc.scalar.copy(
                out=h_once[:].rearrange("p (a c u) -> p a c u", a=HALVES, u=2),
                in_=h_ps[:].rearrange("p (a u c) -> p a c u", a=HALVES, u=2),
            )

        def repeat_h(half):
            h_grouped[half] = keep.tile([P, J_GROUP * P * 2], F32, name="h_grouped%d" % half, align_bytes=64)
            nc.scalar.copy(
                out=h_grouped[half][:].rearrange("p (r w) -> p r w", r=J_GROUP),
                in_=h_once[:, half * 2 * P : (half + 1) * 2 * P].unsqueeze(1).to_broadcast([P, J_GROUP, 2 * P]),
            )

        def repeat_h_codes(half):
            h_mx[half] = mx_operand(keep, COLS, "h_mx%d" % half)
            for once, wide in zip(h_once_mx, h_mx[half]):
                words_once = once[:].bitcast(I32)
                width = words_once.shape[1] // HALVES
                nc.sync.dma_start(
                    out=wide[:].bitcast(I32).rearrange("p (r c) -> p r c", r=J_GROUP),
                    in_=words_once[:, half * width : (half + 1) * width].unsqueeze(1).to_broadcast([P, J_GROUP, width]),
                )

        def quantise_h(half):
            h_mx[half] = mx_operand(keep, COLS, "h_mx%d" % half)
            quantise(nc, h_mx[half], h_grouped[half][:].bitcast(BF16))

        aj_b1 = keep.tile([P, CHUNKS * HALVES * P], F32, name="aj_b1")
        b1_pp = keep.tile([P, CHUNKS], F32, name="b1_pp")

        def compute_aj():
            banks = []
            width = HALVES * P
            for t in range(CHUNKS):
                if t % 2 == 0:
                    banks.append(ps_1.tile([P, 2 * width], F32, name="aj_ps", tag="stage1"))
                part = banks[-1][:, t % 2 * width : (t % 2 + 1) * width]
                mx_pass(nc, part, weights["w_xj"], t * P, (h_once_mx[0][:], h_once_mx[1][:]), True, True)
            for t in range(CHUNKS):
                part = banks[t // 2][:, t % 2 * width : (t % 2 + 1) * width]
                nc.scalar.activation(
                    out=aj_b1[:, t * width : (t + 1) * width], in_=part, func=ACT.Identity, bias=b1_pp[:, t : t + 1]
                )

        base, degrees = [], []

        def compute_degree(half):
            degree = keep.tile([P, 1], F32, name="degree%d" % half)
            degrees.append(degree)
            counted = keep.tile([P, NODES], BF16, name="counted%d" % half)
            nc.scalar.activation(
                out=counted[:], in_=mask_in[:, half * NODES : (half + 1) * NODES], func=ACT.Copy, accum_out=degree[:]
            )

        def compute_base(half):
            rows_base = keep.tile([P, H], F32, name="base%d" % half)
            nc.vector.scalar_tensor_tensor(
                out=rows_base[:], in0=b2_all[:], scalar=degrees[half][:, 0:1], in1=h_sb[half][:], op0=ALU.mult, op1=ALU.add
            )
            base.append(rows_base)

        e_grouped, e_mx, mask_cols, p_ps, pre, r_grouped, r_mx = {}, {}, {}, {}, {}, {}, {}
        out_ps = {}

        def transpose_e(step):
            e_words = e_sb[step][:].bitcast(F32)
            grouped = work.tile([P, COLS * 2], F32, name="e_grouped", align_bytes=64)
            for pair in range(J_GROUP // 2):
                e_ps = ps_t.tile([P, 4 * P], F32, name="e_ps", tag="transposed")
                for block in range(4):
                    word0 = (pair * 4 + block) * P
                    nc.tensor.transpose(e_ps[:, block * P : (block + 1) * P], e_words[:, word0 : word0 + P], ident_f32[:])
                nc.scalar.copy(
                    out=grouped[:, pair * 4 * P : (pair + 1) * 4 * P].rearrange("p (j c u) -> p j c u", j=2, u=2),
                    in_=e_ps[:].rearrange("p (j u c) -> p j c u", j=2, u=2),
                )
            e_grouped[step] = grouped

        def quantise_e(step):
            e_mx[step] = mx_operand(work, COLS, "e_mx")
            quantise(nc, e_mx[step], e_grouped[step][:].bitcast(BF16))

        def lay_out_mask(step):
            half, group = divmod(step, GROUPS)
            if step >= STEPS_MASKED_BY_TENSOR:
                wide_step = step - STEPS_MASKED_BY_TENSOR
                mask_cols[step] = mask_wide[:].bitcast(BF16)[:, wide_step * COLS : (wide_step + 1) * COLS]
                return
            mask_ps = ps_m.tile([P, COLS], BF16, name="mask_ps", tag="mask")
            for j in range(J_GROUP):
                source = group * J_GROUP + j
                nc.tensor.matmul(
                    mask_ps[:, j * P : (j + 1) * P],
                    lhsT=mask_in[:, source : source + 1].to_broadcast([P, P]),
                    rhs=ident_bf16[:],
                    start=True,
                    stop=True,
                )
            cols = work.tile([P, COLS], BF16, name="mask_cols")
            nc.scalar.copy(out=cols[:], in_=mask_ps[:])
            mask_cols[step] = cols[:]

        def stage_1(step):
            half = step // GROUPS
            banks = []
            for t in range(CHUNKS):
                bank = ps_1.tile([P, COLS], F32, name="p_ps", tag="stage1")
                mx_pass(nc, bank[:], weights["w_e2"], t * P, (e_mx[step][0][:], e_mx[step][1][:]), True, False)
                mx_pass(nc, bank[:], weights["w_xi"], t * P, (h_mx[half][0][:], h_mx[half][1][:]), False, True)
                banks.append(bank)
            p_ps[step] = banks

        def scalar_chunks(step):
            return 0 if step == 0 else 2 if step == steps - 2 else 1

        def add_aj_on_scalar(step):
            half, group = divmod(step, GROUPS)
            pre[step] = work.tile([P, CHUNKS * COLS], BF16, name="pre")
            for t in range(scalar_chunks(step)):
                for j in range(J_GROUP):
                    for b in range(GRAPHS_PER_HALF):
                        run = slice((j * GRAPHS_PER_HALF + b) * NODES, (j * GRAPHS_PER_HALF + b + 1) * NODES)
                        source = (t * HALVES + half) * P + b * NODES + group * J_GROUP + j
                        nc.scalar.activation(
                            out=pre[step][:, t * COLS : (t + 1) * COLS][:, run],
                            in_=p_ps[step][t][:, run],
                            func=ACT.Identity,
                            bias=aj_b1[:, source : source + 1],
                        )

        def add_aj(step):
            half, group = divmod(step, GROUPS)
            tile_pre = pre[step]
            for t in range(scalar_chunks(step), CHUNKS):
                aj = aj_b1[:, (t * HALVES + half) * P : (t * HALVES + half + 1) * P]
                nc.vector.tensor_tensor(
                    out=tile_pre[:, t * COLS : (t + 1) * COLS].rearrange("p (j b i) -> p j b i", j=J_GROUP, b=GRAPHS_PER_HALF),
                    in0=p_ps[step][t][:].rearrange("p (j b i) -> p j b i", j=J_GROUP, b=GRAPHS_PER_HALF),
                    in1=aj.rearrange("p (b j) -> p b j", b=GRAPHS_PER_HALF)[:, :, group * J_GROUP : (group + 1) * J_GROUP]
                    .rearrange("p b j -> p j b")
                    .unsqueeze(3)
                    .to_broadcast([P, J_GROUP, GRAPHS_PER_HALF, NODES]),
                    op=ALU.add,
                )

        def apply_mask(step, first, width):
            view = pre[step][:].rearrange("p (t c) -> p t c", t=CHUNKS)[:, :, first : first + width]
            mask = mask_cols[step][:, first : first + width].unsqueeze(1).to_broadcast([P, CHUNKS, width])
            nc.vector.tensor_tensor(out=view, in0=view, in1=mask, op=ALU.mult)

        def regrouping(step, first, width):
            if step not in r_grouped:
                r_grouped[step] = work.tile([P, COLS * PACK], BF16, name="r_grouped", align_bytes=64)
            out_view = r_grouped[step][:, first * PACK : (first + width) * PACK].rearrange("p (c i t) -> p c t i", i=4, t=PACK)
            in_view = pre[step][:].rearrange("p (t c i) -> p c t i", t=PACK, i=4)[:, first // 4 : (first + width) // 4, :, :]
            return out_view, in_view

        def relu_on_scalar(step, first, width):
            out_view, in_view = regrouping(step, first, width)
            nc.scalar.activation(out=out_view, in_=in_view, func=ACT.Relu)

        def relu_on_gpsimd(step, first, width):
            if step not in r_grouped:
                r_grouped[step] = work.tile([P, COLS * PACK], BF16, name="r_grouped", align_bytes=64)
            nc.gpsimd.tensor_scalar(
                out=r_grouped[step][:, first * PACK : (first + width) * PACK].rearrange("p (c t) -> p c t", t=PACK),
                in0=pre[step][:].rearrange("p (t c) -> p c t", t=PACK)[:, first : first + width, :],
                scalar1=0.0,
                scalar2=1.0,
                op0=ALU.max,
                op1=ALU.mult,
            )

        def relu_on_vector(step, first, width):
            out_view, in_view = regrouping(step, first, width)
            nc.vector.tensor_scalar_max(out_view, in_view, 0.0)

        def quantise_r(step, first, width):
            if step not in r_mx:
                r_mx[step] = mx_operand(work, COLS, "r_mx")
            codes, scales = r_mx[step]
            part = slice(first, first + width)
            quantise(nc, (codes[:, part], scales[:, part]), r_grouped[step][:, first * PACK : (first + width) * PACK])

        def stage_2(step, js):
            half, group = divmod(step, GROUPS)
            if half not in out_ps:
                out_ps[half] = (ps_2, ps_m)[half].tile([P, H], F32, name="out_ps%d" % half, tag=("out_ps", "mask")[half])
            for j in js:
                mx_pass(
                    nc,
                    out_ps[half][:],
                    r_mx[step],
                    j * P,
                    (weights["w_m2"][0][:], weights["w_m2"][1][:]),
                    group == 0 and j == 0,
                    group == GROUPS - 1 and j == LAST_J,
                )

        def pipeline_step(s):
            if 0 <= s + 1 < steps:
                add_aj_on_scalar(s + 1)
            if 0 <= s:
                apply_mask(s, 0, COLS)
                if s + 3 < steps:
                    relu_on_gpsimd(s, LAST_J * P, P)
                    relu_on_scalar(s, 0, LAST_J * P)
                else:
                    relu_on_scalar(s, 0, COLS)
            if s == steps - 3:
                for half in range(HALVES):
                    compute_base(half)
            if s + 3 < steps:
                transpose_e(s + 3)
            if 0 <= s + 2 < steps:
                lay_out_mask(s + 2)
            if 0 < s + 2 < steps:
                quantise_e(s + 2)
            if 0 <= s + 1 < steps:
                add_aj(s + 1)
            if s + 2 == 0:
                stage_1(0)
            elif 0 < s + 2 < steps:
                stage_1(s + 2)
            if 0 <= s - 1:
                quantise_r(s - 1, 0, COLS)
                stage_2(s - 1, range(J_GROUP))

        regroup_weight("w_xj", nc.scalar.copy, 0, SCALAR_SHARE)
        transpose_h()
        repeat_h(0)
        b1_ps = ps_2.tile([P, P], BF16, name="b1_ps", tag="out_ps")
        nc.tensor.transpose(b1_ps[:], b1_rows[:], ident_bf16[:])
        regroup_weight("w_xj", nc.vector.tensor_copy, SCALAR_SHARE, H - SCALAR_SHARE)
        quantise_weight("w_xj")
        quantise(nc, h_once_mx, h_once[:].bitcast(BF16))
        nc.vector.tensor_copy(out=b1_pp[:], in_=b1_ps[:, 0:CHUNKS])
        regroup_weight("w_e2", nc.vector.tensor_copy)
        pipeline_step(-3)
        regroup_weight("w_xi", nc.scalar.copy, 0, 4 * H // 16)
        compute_aj()
        quantise_h(0)
        quantise_weight("w_e2")
        regroup_weight("w_xi", nc.vector.tensor_copy, 4 * H // 16, H - 4 * H // 16)
        quantise_e(0)
        quantise_weight("w_xi")
        spread_mask()
        repeat_h_codes(1)
        pipeline_step(-2)
        regroup_weight("w_m2", nc.scalar.copy, 0 * H // 16, 16 * H // 16)
        pipeline_step(-1)
        for half in range(HALVES):
            compute_degree(half)

        def store_result(half, total, pieces):
            width = H // pieces
            for piece in range(pieces):
                part = slice(piece * width, (piece + 1) * width)
                result = work.tile([P, width], F32, name="result%d" % half)
                nc.vector.tensor_tensor(out=result[:], in0=total[:, part], in1=base[half][:, part], op=ALU.add)
                nc.sync.dma_start(out=out_rows[half * P : (half + 1) * P, part], in_=result[:])

        for s in range(steps - 2):
            pipeline_step(s)
            if s == 0:
                quantise_weight("w_m2")

        last = steps - 1
        pair = COLS // 2
        add_aj_on_scalar(last)
        for first in (0, pair):
            apply_mask(last - 1, first, pair)
            relu_on_scalar(last - 1, first, pair)
        quantise_r(last - 2, 0, COLS)
        stage_2(last - 2, range(J_GROUP))
        add_aj(last)
        quantise_r(last - 1, 0, pair)
        stage_2(last - 1, (0, 1))
        apply_mask(last, 0, pair)
        relu_on_scalar(last, 0, P)
        relu_on_scalar(last, P, P)
        quantise_r(last - 1, pair, pair)
        stage_2(last - 1, (2, 3))
        apply_mask(last, pair, pair)
        relu_on_scalar(last, LAST_J * P, P)
        relu_on_vector(last, 2 * P, P)
        for j in range(J_GROUP):
            quantise_r(last, j * P, P)
            stage_2(last, (j,))
        store_result(0, out_ps[0], 1)
        store_result(1, out_ps[1], 2)
